import numpy as np
import ml_dtypes


def mxq(x, axis, fmt="e4m3"):
    dtype, down = {"e4m3": (ml_dtypes.float8_e4m3fn, 7), "e5m2": (ml_dtypes.float8_e5m2, 14)}[fmt]
    v = np.moveaxis(np.asarray(x, np.float32).astype(ml_dtypes.bfloat16).astype(np.float64), axis, -1)
    blocks = v.reshape(v.shape[:-1] + (-1, 32))
    amax = np.abs(blocks).max(-1, keepdims=True)
    byte = np.maximum(np.where(amax > 0, np.frexp(amax)[1] - 1 + 127, 0) - down, 1)
    scale = np.exp2(byte - 127.0)
    codes = (blocks / scale).astype(np.float32).astype(dtype).astype(np.float64)
    return np.moveaxis((codes * scale).reshape(v.shape), -1, axis)


WIDE = False


def mx_kscale(k):
    if not WIDE:
        return np.ones(k)
    levels = np.array([10, -10, 5, -5, 0])
    a = np.random.permutation(np.resize(levels, k // 512 * 4)).reshape(k // 512, 4)
    idx = np.arange(k)
    return np.exp2(a[idx // 512, idx % 128 // 32])


BF16 = ml_dtypes.bfloat16


def bf(x):
    return np.asarray(x, np.float32).astype(BF16)


def f64(x):
    return np.asarray(x).astype(np.float64)


N, C, K, M, HH, WW, CO = 4, 512, 512, 128, 64, 64, 512
P = HH * WW


def setup_inputs():
    s, t = mx_kscale(K), mx_kscale(K)
    return {"h_pix": bf(np.maximum(np.random.standard_normal((N, K, P)), 0.0) * 1.5 * s[None, :, None]),
            "wp2": bf(np.random.standard_normal((K, K)) * np.sqrt(2.0 / K) * t[:, None] / s[None, :]),
            "sp2": bf(np.random.uniform(0.5, 1.5, K)),
            "bp2": bf(np.random.standard_normal(K) * 0.2 * t),
            "key_obj": bf(np.maximum(np.random.standard_normal((N, K, M)), 0.0) * 1.5 / t[None, :, None])}


def reference(h_pix, wp2, sp2, bp2, key_obj):
    y = mxq(f64(wp2), 1, "e4m3") @ mxq(f64(h_pix), 1, "e4m3")
    query = np.maximum(y * f64(sp2)[None, :, None] + f64(bp2)[None, :, None], 0.0)
    sim = (mxq(query, 1, "e4m3").transpose(0, 2, 1) @ mxq(f64(key_obj), 1, "e4m3")) * (K ** -0.5)
    e = np.exp(sim - sim.max(-1, keepdims=True))
    return e / e.sum(-1, keepdims=True)

@@ -1,0 +1,249 @@
+from contextlib import ExitStack
+
+import concourse.mybir as mybir
+from concourse.masks import make_identity
+
+F32 = mybir.dt.float32
+BF16 = mybir.dt.bfloat16
+U32 = mybir.dt.uint32
+U8 = mybir.dt.uint8
+FP8X4 = mybir.dt.float8_e4m3fn_x4
+ACT = mybir.ActivationFunctionType
+ALU = mybir.AluOpType
+AXIS = mybir.AxisListType
+
+P = 128
+PACK = 4
+IMAGES = 4
+CHANNELS = P * PACK
+PIXELS = 4096
+REGIONS = 128
+CHUNK = 512
+TILES = CHUNK // P
+CHUNKS = IMAGES * PIXELS // CHUNK
+RUN = 4
+SCALAR_COLUMNS = 224
+CHUNKS_PER_IMAGE = PIXELS // CHUNK
+SIM_SCALE = CHANNELS ** -0.5
+
+FLOPS = 2 * IMAGES * PIXELS * CHANNELS * (CHANNELS + REGIONS)
+
+
+def regroup(copy, grouped, rows):
+    copy(
+        out=grouped.rearrange("p (c i) j -> p c j i", i=RUN),
+        in_=rows.rearrange("p j (c i) -> p c j i", i=RUN),
+    )
+
+
+def tile_spatialocr_module_pa_t_kernel(tc, h_pix, wp2, sp2, bp2, key_obj, out):
+    nc = tc.nc
+    with ExitStack() as ctx:
+        keep = ctx.enter_context(tc.tile_pool(name="keep", bufs=1))
+        work = ctx.enter_context(tc.tile_pool(name="work", bufs=3))
+        small = ctx.enter_context(tc.tile_pool(name="small", bufs=4))
+        y_banks = ctx.enter_context(tc.psum_pool(name="y_banks", bufs=6))
+        sim_banks = ctx.enter_context(tc.psum_pool(name="sim_banks", bufs=2))
+        ctx.enter_context(tc.manual_schedule())
+
+        w_rows = keep.tile([P, PACK * CHANNELS], BF16)
+        nc.scalar.dma_start(out=w_rows[:], in_=wp2.rearrange("(p t) k -> p (t k)", t=PACK))
+        gain_bf = keep.tile([P, PACK], BF16)
+        nc.scalar.dma_start(out=gain_bf[:], in_=sp2.rearrange("(p t) -> p t", t=PACK))
+        shift_bf = keep.tile([P, PACK], BF16)
+        nc.scalar.dma_start(out=shift_bf[:], in_=bp2.rearrange("(p t) -> p t", t=PACK))
+        key_rows = keep.tile([P, IMAGES, PACK, REGIONS], BF16)
+        nc.scalar.dma_start(out=key_rows[:], in_=key_obj.rearrange("n (p t) m -> p n t m", t=PACK))
+
+        h_rows = []
+        for c in range(CHUNKS):
+            n, first = divmod(c * CHUNK, PIXELS)
+            rows = keep.tile([P, PACK, CHUNK], BF16, name="h_rows_%d" % c)
+            nc.sync.dma_start(
+                out=rows[:],
+                in_=h_pix[n, :, first : first + CHUNK].rearrange("(p j) w -> p j w", j=PACK),
+            )
+            h_rows.append(rows)
+
+        ident = keep.tile([P, P], F32)
+        make_identity(nc, ident[:])
+        gain = keep.tile([P, PACK], F32)
+        nc.gpsimd.tensor_copy(out=gain[:], in_=gain_bf[:])
+        shift = keep.tile([P, PACK], F32)
+        nc.gpsimd.tensor_copy(out=shift[:], in_=shift_bf[:])
+
+        live = {}
+
+        def h_regroup_scalar(c):
+            h_grouped = work.tile([P, CHUNK, PACK], BF16, align_bytes=64)
+            split = CHUNK - SCALAR_COLUMNS
+            regroup(nc.scalar.copy, h_grouped[:, split:, :], h_rows[c][:, :, split:])
+            live["h_grouped", c] = h_grouped
+
+        def h_regroup_vector(c):
+            split = CHUNK - SCALAR_COLUMNS
+            regroup(nc.vector.tensor_copy, live["h_grouped", c][:, :split, :], h_rows[c][:, :, :split])
+
+        def h_quantise(c):
+            h_codes = work.tile([P, CHUNK], U32, align_bytes=64)
+            h_scales = work.tile([P, CHUNK], U8, align_bytes=64)
+            nc.vector.quantize_mx(
+                out=h_codes[:].bitcast(FP8X4),
+                scales=h_scales[:],
+                in_=live.pop(("h_grouped", c))[:].rearrange("p w j -> p (w j)"),
+            )
+            live["h_mx", c] = (h_codes, h_scales)
+
+        def w_quantise():
+            w_words = w_rows[:].bitcast(F32).rearrange("p (t q u) -> p t u q", t=PACK, u=2)
+            w_grouped = keep.tile([P, PACK * P * PACK], BF16, align_bytes=64)
+            w_grouped_words = w_grouped[:].bitcast(F32).rearrange("p (t o u) -> p t o u", t=PACK, u=2)
+            for half in range(2):
+                w_t = sim_banks.tile([P, 2, 2, P], F32, tag="sim")
+                for t in range(2):
+                    for u in range(2):
+                        nc.tensor.transpose(w_t[:, t, u, :], w_words[:, 2 * half + t, u, :], ident[:])
+                nc.vector.tensor_copy(
+                    out=w_grouped_words[:, 2 * half : 2 * half + 2, :, :],
+                    in_=w_t[:].rearrange("p t u o -> p t o u"),
+                )
+            w_codes = keep.tile([P, PACK * P], U32, align_bytes=64)
+            w_scales = keep.tile([P, PACK * P], U8, align_bytes=64)
+            nc.vector.quantize_mx(out=w_codes[:].bitcast(FP8X4), scales=w_scales[:], in_=w_grouped[:])
+            live["w_mx"] = (w_codes, w_scales)
+
+        def project(c):
+            if c == 0:
+                w_quantise()
+            w_codes, w_scales = live["w_mx"]
+            h_codes, h_scales = live.pop(("h_mx", c))
+            for t in range(PACK):
+                y = y_banks.tile([P, CHUNK], F32)
+                nc.tensor.matmul_mx(
+                    out=y[:],
+                    lhsT=w_codes[:, t * P : (t + 1) * P].bitcast(FP8X4),
+                    lhsT_scale=w_scales[:, t * P : (t + 1) * P],
+                    rhs=h_codes[:].bitcast(FP8X4),
+                    rhs_scale=h_scales[:],
+                    start=True,
+                    stop=True,
+                )
+                live["y", c, t] = y
+
+        def leave_psum(c):
+            q_rows = work.tile([P, PACK, CHUNK], BF16)
+            for t in range(PACK):
+                nc.scalar.activation(
+                    out=q_rows[:, t, :],
+                    in_=live.pop(("y", c, t))[:],
+                    func=ACT.Relu,
+                    bias=shift[:, t : t + 1],
+                    scale=gain[:, t : t + 1],
+                )
+            live["q_rows", c] = q_rows
+
+        def key_quantise(n):
+            key_grouped = work.tile([P, REGIONS, PACK], BF16, align_bytes=64)
+            nc.vector.tensor_copy(out=key_grouped[:], in_=key_rows[:, n, :, :].rearrange("p t m -> p m t"))
+            key_codes = work.tile([P, REGIONS], U32, align_bytes=64)
+            key_scales = work.tile([P, REGIONS], U8, align_bytes=64)
+            nc.vector.quantize_mx(
+                out=key_codes[:].bitcast(FP8X4),
+                scales=key_scales[:],
+                in_=key_grouped[:].rearrange("p m t -> p (m t)"),
+            )
+            live["key_mx"] = (key_codes, key_scales)
+
+        def q_regroup(c):
+            q_grouped = work.tile([P, CHUNK, PACK], BF16, align_bytes=64)
+            regroup(nc.vector.tensor_copy, q_grouped[:], live.pop(("q_rows", c))[:])
+            live["q_grouped", c] = q_grouped
+
+        def q_quantise(c):
+            q_codes = work.tile([P, CHUNK], U32, align_bytes=64)
+            q_scales = work.tile([P, CHUNK], U8, align_bytes=64)
+            nc.vector.quantize_mx(
+                out=q_codes[:].bitcast(FP8X4),
+                scales=q_scales[:],
+                in_=live.pop(("q_grouped", c))[:].rearrange("p w j -> p (w j)"),
+            )
+            live["q_mx", c] = (q_codes, q_scales)
+
+        def scores(c):
+            if c % CHUNKS_PER_IMAGE == 0:
+                key_quantise(c // CHUNKS_PER_IMAGE)
+            key_codes, key_scales = live["key_mx"]
+            q_codes, q_scales = live.pop(("q_mx", c))
+            sim = sim_banks.tile([P, TILES, REGIONS], F32, tag="sim")
+            for i in range(TILES):
+                nc.tensor.matmul_mx(
+                    out=sim[:, i, :],
+                    lhsT=q_codes[:, i * P : (i + 1) * P].bitcast(FP8X4),
+                    lhsT_scale=q_scales[:, i * P : (i + 1) * P],
+                    rhs=key_codes[:].bitcast(FP8X4),
+                    rhs_scale=key_scales[:],
+                    start=True,
+                    stop=True,
+                )
+            live["sim", c] = sim
+
+        def row_max(c):
+            top = small.tile([P, TILES], F32)
+            nc.vector.tensor_reduce(out=top[:], in_=live["sim", c][:], axis=AXIS.X, op=ALU.max)
+            live["top", c] = top
+
+        def row_shift(c):
+            minus_top = small.tile([P, TILES], F32)
+            nc.vector.tensor_scalar_mul(out=minus_top[:], in0=live.pop(("top", c))[:], scalar1=-SIM_SCALE)
+            live["minus_top", c] = minus_top
+
+        def exponent(c):
+            sim = live.pop(("sim", c))
+            minus_top = live.pop(("minus_top", c))
+            e = work.tile([P, TILES, REGIONS], F32)
+            sums = small.tile([P, TILES], F32)
+            for i in range(TILES):
+                nc.scalar.activation(
+                    out=e[:, i, :],
+                    in_=sim[:, i, :],
+                    func=ACT.Exp,
+                    bias=minus_top[:, i : i + 1],
+                    scale=SIM_SCALE,
+                    accum_out=sums[:, i : i + 1],
+                )
+            live["e", c] = e
+            live["sums", c] = sums
+
+        def invert_sums(c):
+            inverse = small.tile([P, TILES], F32)
+            nc.vector.reciprocal(out=inverse[:], in_=live.pop(("sums", c))[:])
+            live["inverse", c] = inverse
+
+        def normalise(c):
+            n, first = divmod(c * CHUNK, PIXELS)
+            e = live.pop(("e", c))
+            inverse = live.pop(("inverse", c))
+            for i in range(TILES):
+                nc.vector.tensor_scalar_mul(out=e[:, i, :], in0=e[:, i, :], scalar1=inverse[:, i : i + 1])
+            nc.sync.dma_start(
+                out=out[n, first : first + CHUNK, :].rearrange("(i p) m -> p i m", p=P), in_=e[:]
+            )
+
+        def at(stage, c):
+            if 0 <= c < CHUNKS:
+                stage(c)
+
+        for s in range(CHUNKS + 5):
+            at(row_max, s - 4)
+            at(leave_psum, s - 2)
+            at(q_regroup, s - 3)
+            at(row_shift, s - 4)
+            at(h_regroup_vector, s - 1)
+            at(invert_sums, s - 5)
+            at(q_quantise, s - 3)
+            at(scores, s - 3)
+            at(h_quantise, s - 1)
+            at(project, s - 1)
+            at(h_regroup_scalar, s)
+            at(exponent, s - 4)
+            at(normalise, s - 5)

@@ -22,8 +22,9 @@ CHUNK = 512
 TILES = CHUNK // P
 CHUNKS = IMAGES * PIXELS // CHUNK
 RUN = 4
-SCALAR_COLUMNS = 224
+SCALAR_COLUMNS = 192
 CHUNKS_PER_IMAGE = PIXELS // CHUNK
+LEAD = 8
 SIM_SCALE = CHANNELS ** -0.5
 
 FLOPS = 2 * IMAGES * PIXELS * CHANNELS * (CHANNELS + REGIONS)
@@ -40,6 +41,7 @@ def tile_spatialocr_module_pa_t_kernel(tc, h_pix, wp2, sp2, bp2, key_obj, out):
     nc = tc.nc
     with ExitStack() as ctx:
         keep = ctx.enter_context(tc.tile_pool(name="keep", bufs=1))
+        stream = ctx.enter_context(tc.tile_pool(name="stream", bufs=LEAD + 2))
         work = ctx.enter_context(tc.tile_pool(name="work", bufs=3))
         small = ctx.enter_context(tc.tile_pool(name="small", bufs=4))
         y_banks = ctx.enter_context(tc.psum_pool(name="y_banks", bufs=6))
@@ -55,16 +57,6 @@ def tile_spatialocr_module_pa_t_kernel(tc, h_pix, wp2, sp2, bp2, key_obj, out):
         key_rows = keep.tile([P, IMAGES, PACK, REGIONS], BF16)
         nc.scalar.dma_start(out=key_rows[:], in_=key_obj.rearrange("n (p t) m -> p n t m", t=PACK))
 
-        h_rows = []
-        for c in range(CHUNKS):
-            n, first = divmod(c * CHUNK, PIXELS)
-            rows = keep.tile([P, PACK, CHUNK], BF16, name="h_rows_%d" % c)
-            nc.sync.dma_start(
-                out=rows[:],
-                in_=h_pix[n, :, first : first + CHUNK].rearrange("(p j) w -> p j w", j=PACK),
-            )
-            h_rows.append(rows)
-
         ident = keep.tile([P, P], F32)
         make_identity(nc, ident[:])
         gain = keep.tile([P, PACK], F32)
@@ -74,15 +66,25 @@ def tile_spatialocr_module_pa_t_kernel(tc, h_pix, wp2, sp2, bp2, key_obj, out):
 
         live = {}
 
+        def load(c):
+            n, first = divmod(c * CHUNK, PIXELS)
+            h_rows = stream.tile([P, PACK, CHUNK], BF16)
+            nc.sync.dma_start(
+                out=h_rows[:],
+                in_=h_pix[n, :, first : first + CHUNK].rearrange("(p j) w -> p j w", j=PACK),
+            )
+            live["h_rows", c] = h_rows
+
         def h_regroup_scalar(c):
             h_grouped = work.tile([P, CHUNK, PACK], BF16, align_bytes=64)
             split = CHUNK - SCALAR_COLUMNS
-            regroup(nc.scalar.copy, h_grouped[:, split:, :], h_rows[c][:, :, split:])
+            regroup(nc.scalar.copy, h_grouped[:, split:, :], live["h_rows", c][:, :, split:])
             live["h_grouped", c] = h_grouped
 
         def h_regroup_vector(c):
             split = CHUNK - SCALAR_COLUMNS
-            regroup(nc.vector.tensor_copy, live["h_grouped", c][:, :split, :], h_rows[c][:, :, :split])
+            h_rows = live.pop(("h_rows", c))
+            regroup(nc.vector.tensor_copy, live["h_grouped", c][:, :split, :], h_rows[:, :, :split])
 
         def h_quantise(c):
             h_codes = work.tile([P, CHUNK], U32, align_bytes=64)
@@ -233,7 +235,10 @@ def tile_spatialocr_module_pa_t_kernel(tc, h_pix, wp2, sp2, bp2, key_obj, out):
             if 0 <= c < CHUNKS:
                 stage(c)
 
+        for c in range(LEAD):
+            load(c)
         for s in range(CHUNKS + 5):
+            at(load, s + LEAD)
             at(row_max, s - 4)
             at(leave_psum, s - 2)
             at(q_regroup, s - 3)

@@ -22,7 +22,6 @@ CHUNK = 512
 TILES = CHUNK // P
 CHUNKS = IMAGES * PIXELS // CHUNK
 RUN = 4
-SCALAR_COLUMNS = 192
 CHUNKS_PER_IMAGE = PIXELS // CHUNK
 LEAD = 8
 SIM_SCALE = CHANNELS ** -0.5
@@ -43,6 +42,7 @@ def tile_spatialocr_module_pa_t_kernel(tc, h_pix, wp2, sp2, bp2, key_obj, out):
         keep = ctx.enter_context(tc.tile_pool(name="keep", bufs=1))
         stream = ctx.enter_context(tc.tile_pool(name="stream", bufs=LEAD + 2))
         work = ctx.enter_context(tc.tile_pool(name="work", bufs=3))
+        result = ctx.enter_context(tc.tile_pool(name="result", bufs=5))
         small = ctx.enter_context(tc.tile_pool(name="small", bufs=4))
         y_banks = ctx.enter_context(tc.psum_pool(name="y_banks", bufs=6))
         sim_banks = ctx.enter_context(tc.psum_pool(name="sim_banks", bufs=2))
@@ -75,16 +75,10 @@ def tile_spatialocr_module_pa_t_kernel(tc, h_pix, wp2, sp2, bp2, key_obj, out):
             )
             live["h_rows", c] = h_rows
 
-        def h_regroup_scalar(c):
+        def h_regroup(c):
             h_grouped = work.tile([P, CHUNK, PACK], BF16, align_bytes=64)
-            split = CHUNK - SCALAR_COLUMNS
-            regroup(nc.scalar.copy, h_grouped[:, split:, :], live["h_rows", c][:, :, split:])
+            regroup(nc.vector.tensor_copy, h_grouped[:], live.pop(("h_rows", c))[:])
             live["h_grouped", c] = h_grouped
-
-        def h_regroup_vector(c):
-            split = CHUNK - SCALAR_COLUMNS
-            h_rows = live.pop(("h_rows", c))
-            regroup(nc.vector.tensor_copy, live["h_grouped", c][:, :split, :], h_rows[:, :, :split])
 
         def h_quantise(c):
             h_codes = work.tile([P, CHUNK], U32, align_bytes=64)
@@ -98,20 +92,20 @@ def tile_spatialocr_module_pa_t_kernel(tc, h_pix, wp2, sp2, bp2, key_obj, out):
 
         def w_quantise():
             w_words = w_rows[:].bitcast(F32).rearrange("p (t q u) -> p t u q", t=PACK, u=2)
-            w_grouped = keep.tile([P, PACK * P * PACK], BF16, align_bytes=64)
-            w_grouped_words = w_grouped[:].bitcast(F32).rearrange("p (t o u) -> p t o u", t=PACK, u=2)
-            for half in range(2):
-                w_t = sim_banks.tile([P, 2, 2, P], F32, tag="sim")
-                for t in range(2):
-                    for u in range(2):
-                        nc.tensor.transpose(w_t[:, t, u, :], w_words[:, 2 * half + t, u, :], ident[:])
+            w_grouped = keep.tile([P, PACK, P * PACK], BF16, align_bytes=64)
+            w_codes = keep.tile([P, PACK, P], U32, align_bytes=64)
+            w_scales = keep.tile([P, PACK, P], U8, align_bytes=64)
+            for t in range(PACK):
+                w_t = sim_banks.tile([P, 2, P], F32, tag="sim")
+                for u in range(2):
+                    nc.tensor.transpose(w_t[:, u, :], w_words[:, t, u, :], ident[:])
                 nc.vector.tensor_copy(
-                    out=w_grouped_words[:, 2 * half : 2 * half + 2, :, :],
-                    in_=w_t[:].rearrange("p t u o -> p t o u"),
+                    out=w_grouped[:, t, :].bitcast(F32).rearrange("p (o u) -> p o u", u=2),
+                    in_=w_t[:].rearrange("p u o -> p o u"),
                 )
-            w_codes = keep.tile([P, PACK * P], U32, align_bytes=64)
-            w_scales = keep.tile([P, PACK * P], U8, align_bytes=64)
-            nc.vector.quantize_mx(out=w_codes[:].bitcast(FP8X4), scales=w_scales[:], in_=w_grouped[:])
+                nc.vector.quantize_mx(
+                    out=w_codes[:, t, :].bitcast(FP8X4), scales=w_scales[:, t, :], in_=w_grouped[:, t, :]
+                )
             live["w_mx"] = (w_codes, w_scales)
 
         def project(c):
@@ -123,8 +117,8 @@ def tile_spatialocr_module_pa_t_kernel(tc, h_pix, wp2, sp2, bp2, key_obj, out):
                 y = y_banks.tile([P, CHUNK], F32)
                 nc.tensor.matmul_mx(
                     out=y[:],
-                    lhsT=w_codes[:, t * P : (t + 1) * P].bitcast(FP8X4),
-                    lhsT_scale=w_scales[:, t * P : (t + 1) * P],
+                    lhsT=w_codes[:, t, :].bitcast(FP8X4),
+                    lhsT_scale=w_scales[:, t, :],
                     rhs=h_codes[:].bitcast(FP8X4),
                     rhs_scale=h_scales[:],
                     start=True,
@@ -202,7 +196,7 @@ def tile_spatialocr_module_pa_t_kernel(tc, h_pix, wp2, sp2, bp2, key_obj, out):
         def exponent(c):
             sim = live.pop(("sim", c))
             minus_top = live.pop(("minus_top", c))
-            e = work.tile([P, TILES, REGIONS], F32)
+            e = result.tile([P, TILES, REGIONS], F32)
             sums = small.tile([P, TILES], F32)
             for i in range(TILES):
                 nc.scalar.activation(
@@ -226,7 +220,7 @@ def tile_spatialocr_module_pa_t_kernel(tc, h_pix, wp2, sp2, bp2, key_obj, out):
             e = live.pop(("e", c))
             inverse = live.pop(("inverse", c))
             for i in range(TILES):
-                nc.vector.tensor_scalar_mul(out=e[:, i, :], in0=e[:, i, :], scalar1=inverse[:, i : i + 1])
+                nc.scalar.activation(out=e[:, i, :], in_=e[:, i, :], func=ACT.Copy, scale=inverse[:, i : i + 1])
             nc.sync.dma_start(
                 out=out[n, first : first + CHUNK, :].rearrange("(i p) m -> p i m", p=P), in_=e[:]
             )
@@ -239,16 +233,15 @@ def tile_spatialocr_module_pa_t_kernel(tc, h_pix, wp2, sp2, bp2, key_obj, out):
             load(c)
         for s in range(CHUNKS + 5):
             at(load, s + LEAD)
-            at(row_max, s - 4)
-            at(leave_psum, s - 2)
-            at(q_regroup, s - 3)
-            at(row_shift, s - 4)
-            at(h_regroup_vector, s - 1)
-            at(invert_sums, s - 5)
-            at(q_quantise, s - 3)
-            at(scores, s - 3)
-            at(h_quantise, s - 1)
-            at(project, s - 1)
-            at(h_regroup_scalar, s)
-            at(exponent, s - 4)
+            at(leave_psum, s - 1)
+            at(q_regroup, s - 2)
+            at(row_max, s - 3)
+            at(h_regroup, s)
+            at(row_shift, s - 3)
+            at(q_quantise, s - 2)
+            at(scores, s - 2)
+            at(invert_sums, s - 4)
+            at(h_quantise, s)
+            at(project, s)
             at(normalise, s - 5)
+            at(exponent, s - 3)

@@ -21,16 +21,23 @@ REGIONS = 128
 CHUNK = 512
 TILES = CHUNK // P
 CHUNKS = IMAGES * PIXELS // CHUNK
-RUN = 4
 CHUNKS_PER_IMAGE = PIXELS // CHUNK
-LEAD = 8
+RUN = 4
 SIM_SCALE = CHANNELS ** -0.5
+
+LEAD = 8
+DEPTH = 5
+WORK_BUFS = 3
+RESULT_BUFS = 5
+SMALL_BUFS = 4
+Y_BANKS = 6
+SIM_BANKS = 2
 
 FLOPS = 2 * IMAGES * PIXELS * CHANNELS * (CHANNELS + REGIONS)
 
 
-def regroup(copy, grouped, rows):
-    copy(
+def regroup(nc, grouped, rows):
+    nc.vector.tensor_copy(
         out=grouped.rearrange("p (c i) j -> p c j i", i=RUN),
         in_=rows.rearrange("p j (c i) -> p c j i", i=RUN),
     )
@@ -41,11 +48,11 @@ def tile_spatialocr_module_pa_t_kernel(tc, h_pix, wp2, sp2, bp2, key_obj, out):
     with ExitStack() as ctx:
         keep = ctx.enter_context(tc.tile_pool(name="keep", bufs=1))
         stream = ctx.enter_context(tc.tile_pool(name="stream", bufs=LEAD + 2))
-        work = ctx.enter_context(tc.tile_pool(name="work", bufs=3))
-        result = ctx.enter_context(tc.tile_pool(name="result", bufs=5))
-        small = ctx.enter_context(tc.tile_pool(name="small", bufs=4))
-        y_banks = ctx.enter_context(tc.psum_pool(name="y_banks", bufs=6))
-        sim_banks = ctx.enter_context(tc.psum_pool(name="sim_banks", bufs=2))
+        work = ctx.enter_context(tc.tile_pool(name="work", bufs=WORK_BUFS))
+        result = ctx.enter_context(tc.tile_pool(name="result", bufs=RESULT_BUFS))
+        small = ctx.enter_context(tc.tile_pool(name="small", bufs=SMALL_BUFS))
+        y_banks = ctx.enter_context(tc.psum_pool(name="y_banks", bufs=Y_BANKS))
+        sim_banks = ctx.enter_context(tc.psum_pool(name="sim_banks", bufs=SIM_BANKS))
         ctx.enter_context(tc.manual_schedule())
 
         w_rows = keep.tile([P, PACK * CHANNELS], BF16)
@@ -55,7 +62,7 @@ def tile_spatialocr_module_pa_t_kernel(tc, h_pix, wp2, sp2, bp2, key_obj, out):
         shift_bf = keep.tile([P, PACK], BF16)
         nc.scalar.dma_start(out=shift_bf[:], in_=bp2.rearrange("(p t) -> p t", t=PACK))
         key_rows = keep.tile([P, IMAGES, PACK, REGIONS], BF16)
-        nc.scalar.dma_start(out=key_rows[:], in_=key_obj.rearrange("n (p t) m -> p n t m", t=PACK))
+        nc.scalar.dma_start(out=key_rows[:], in_=key_obj.rearrange("n (p j) m -> p n j m", j=PACK))
 
         ident = keep.tile([P, P], F32)
         make_identity(nc, ident[:])
@@ -77,7 +84,7 @@ def tile_spatialocr_module_pa_t_kernel(tc, h_pix, wp2, sp2, bp2, key_obj, out):
 
         def h_regroup(c):
             h_grouped = work.tile([P, CHUNK, PACK], BF16, align_bytes=64)
-            regroup(nc.vector.tensor_copy, h_grouped[:], live.pop(("h_rows", c))[:])
+            regroup(nc, h_grouped[:], live.pop(("h_rows", c))[:])
             live["h_grouped", c] = h_grouped
 
         def h_quantise(c):
@@ -138,21 +145,9 @@ def tile_spatialocr_module_pa_t_kernel(tc, h_pix, wp2, sp2, bp2, key_obj, out):
                 )
             live["q_rows", c] = q_rows
 
-        def key_quantise(n):
-            key_grouped = work.tile([P, REGIONS, PACK], BF16, align_bytes=64)
-            nc.vector.tensor_copy(out=key_grouped[:], in_=key_rows[:, n, :, :].rearrange("p t m -> p m t"))
-            key_codes = work.tile([P, REGIONS], U32, align_bytes=64)
-            key_scales = work.tile([P, REGIONS], U8, align_bytes=64)
-            nc.vector.quantize_mx(
-                out=key_codes[:].bitcast(FP8X4),
-                scales=key_scales[:],
-                in_=key_grouped[:].rearrange("p m t -> p (m t)"),
-            )
-            live["key_mx"] = (key_codes, key_scales)
-
         def q_regroup(c):
             q_grouped = work.tile([P, CHUNK, PACK], BF16, align_bytes=64)
-            regroup(nc.vector.tensor_copy, q_grouped[:], live.pop(("q_rows", c))[:])
+            regroup(nc, q_grouped[:], live.pop(("q_rows", c))[:])
             live["q_grouped", c] = q_grouped
 
         def q_quantise(c):
@@ -164,6 +159,18 @@ def tile_spatialocr_module_pa_t_kernel(tc, h_pix, wp2, sp2, bp2, key_obj, out):
                 in_=live.pop(("q_grouped", c))[:].rearrange("p w j -> p (w j)"),
             )
             live["q_mx", c] = (q_codes, q_scales)
+
+        def key_quantise(n):
+            key_grouped = work.tile([P, REGIONS, PACK], BF16, align_bytes=64)
+            regroup(nc, key_grouped[:], key_rows[:, n, :, :])
+            key_codes = work.tile([P, REGIONS], U32, align_bytes=64)
+            key_scales = work.tile([P, REGIONS], U8, align_bytes=64)
+            nc.vector.quantize_mx(
+                out=key_codes[:].bitcast(FP8X4),
+                scales=key_scales[:],
+                in_=key_grouped[:].rearrange("p m j -> p (m j)"),
+            )
+            live["key_mx"] = (key_codes, key_scales)
 
         def scores(c):
             if c % CHUNKS_PER_IMAGE == 0:
@@ -231,7 +238,7 @@ def tile_spatialocr_module_pa_t_kernel(tc, h_pix, wp2, sp2, bp2, key_obj, out):
 
         for c in range(LEAD):
             load(c)
-        for s in range(CHUNKS + 5):
+        for s in range(CHUNKS + DEPTH):
             at(load, s + LEAD)
             at(leave_psum, s - 1)
             at(q_regroup, s - 2)
@@ -243,5 +250,5 @@ def tile_spatialocr_module_pa_t_kernel(tc, h_pix, wp2, sp2, bp2, key_obj, out):
             at(invert_sums, s - 4)
             at(h_quantise, s)
             at(project, s)
-            at(normalise, s - 5)
+            at(normalise, s - DEPTH)
             at(exponent, s - 3)

@@ -22,16 +22,19 @@ CHUNK = 512
 TILES = CHUNK // P
 CHUNKS = IMAGES * PIXELS // CHUNK
 CHUNKS_PER_IMAGE = PIXELS // CHUNK
+GROUP = 2
 RUN = 4
 SIM_SCALE = CHANNELS ** -0.5
 
-LEAD = 8
+GROUPS = [[0]] + [[c, c + 1] for c in range(1, CHUNKS - 1, GROUP)] + [[CHUNKS - 1]]
+
+LEAD = 4
 DEPTH = 5
 WORK_BUFS = 3
-RESULT_BUFS = 5
+RESULT_BUFS = 4
 SMALL_BUFS = 4
-Y_BANKS = 6
-SIM_BANKS = 2
+Y_BANKS = 4
+SIM_BANKS = 4
 
 FLOPS = 2 * IMAGES * PIXELS * CHANNELS * (CHANNELS + REGIONS)
 
@@ -61,8 +64,9 @@ def tile_spatialocr_module_pa_t_kernel(tc, h_pix, wp2, sp2, bp2, key_obj, out):
         nc.scalar.dma_start(out=gain_bf[:], in_=sp2.rearrange("(p t) -> p t", t=PACK))
         shift_bf = keep.tile([P, PACK], BF16)
         nc.scalar.dma_start(out=shift_bf[:], in_=bp2.rearrange("(p t) -> p t", t=PACK))
-        key_rows = keep.tile([P, IMAGES, PACK, REGIONS], BF16)
-        nc.scalar.dma_start(out=key_rows[:], in_=key_obj.rearrange("n (p j) m -> p n j m", j=PACK))
+        key_rows = keep.tile([P, PACK, IMAGES, REGIONS], BF16)
+        for n in range(IMAGES):
+            nc.scalar.dma_start(out=key_rows[:, :, n, :], in_=key_obj[n].rearrange("(p j) m -> p j m", j=PACK))
 
         ident = keep.tile([P, P], F32)
         make_identity(nc, ident[:])
@@ -73,29 +77,35 @@ def tile_spatialocr_module_pa_t_kernel(tc, h_pix, wp2, sp2, bp2, key_obj, out):
 
         live = {}
 
-        def load(c):
-            n, first = divmod(c * CHUNK, PIXELS)
-            h_rows = stream.tile([P, PACK, CHUNK], BF16)
-            nc.sync.dma_start(
-                out=h_rows[:],
-                in_=h_pix[n, :, first : first + CHUNK].rearrange("(p j) w -> p j w", j=PACK),
-            )
-            live["h_rows", c] = h_rows
+        def load(g):
+            chunks = GROUPS[g]
+            h_rows = stream.tile([P, PACK, len(chunks) * CHUNK], BF16)
+            for n in sorted({c // CHUNKS_PER_IMAGE for c in chunks}):
+                mine = [c for c in chunks if c // CHUNKS_PER_IMAGE == n]
+                first = mine[0] % CHUNKS_PER_IMAGE * CHUNK
+                at_column = (mine[0] - chunks[0]) * CHUNK
+                width = len(mine) * CHUNK
+                nc.sync.dma_start(
+                    out=h_rows[:, :, at_column : at_column + width],
+                    in_=h_pix[n, :, first : first + width].rearrange("(p j) w -> p j w", j=PACK),
+                )
+            live["h_rows", g] = h_rows
 
-        def h_regroup(c):
-            h_grouped = work.tile([P, CHUNK, PACK], BF16, align_bytes=64)
-            regroup(nc, h_grouped[:], live.pop(("h_rows", c))[:])
-            live["h_grouped", c] = h_grouped
+        def h_regroup(g):
+            h_grouped = work.tile([P, len(GROUPS[g]) * CHUNK, PACK], BF16, align_bytes=64)
+            regroup(nc, h_grouped[:], live.pop(("h_rows", g))[:])
+            live["h_grouped", g] = h_grouped
 
-        def h_quantise(c):
-            h_codes = work.tile([P, CHUNK], U32, align_bytes=64)
-            h_scales = work.tile([P, CHUNK], U8, align_bytes=64)
+        def h_quantise(g):
+            width = len(GROUPS[g]) * CHUNK
+            h_codes = work.tile([P, width], U32, align_bytes=64)
+            h_scales = work.tile([P, width], U8, align_bytes=64)
             nc.vector.quantize_mx(
                 out=h_codes[:].bitcast(FP8X4),
                 scales=h_scales[:],
-                in_=live.pop(("h_grouped", c))[:].rearrange("p w j -> p (w j)"),
+                in_=live.pop(("h_grouped", g))[:].rearrange("p w j -> p (w j)"),
             )
-            live["h_mx", c] = (h_codes, h_scales)
+            live["h_mx", g] = (h_codes, h_scales)
 
         def w_quantise():
             w_words = w_rows[:].bitcast(F32).rearrange("p (t q u) -> p t u q", t=PACK, u=2)
@@ -115,140 +125,167 @@ def tile_spatialocr_module_pa_t_kernel(tc, h_pix, wp2, sp2, bp2, key_obj, out):
                 )
             live["w_mx"] = (w_codes, w_scales)
 
-        def project(c):
-            if c == 0:
+        def project(g):
+            if g == 0:
                 w_quantise()
             w_codes, w_scales = live["w_mx"]
-            h_codes, h_scales = live.pop(("h_mx", c))
-            for t in range(PACK):
-                y = y_banks.tile([P, CHUNK], F32)
-                nc.tensor.matmul_mx(
-                    out=y[:],
-                    lhsT=w_codes[:, t, :].bitcast(FP8X4),
-                    lhsT_scale=w_scales[:, t, :],
-                    rhs=h_codes[:].bitcast(FP8X4),
-                    rhs_scale=h_scales[:],
-                    start=True,
-                    stop=True,
-                )
-                live["y", c, t] = y
+            h_codes, h_scales = live.pop(("h_mx", g))
+            for k, c in enumerate(GROUPS[g]):
+                columns = slice(k * CHUNK, (k + 1) * CHUNK)
+                for t in range(PACK):
+                    y = y_banks.tile([P, CHUNK], F32)
+                    nc.tensor.matmul_mx(
+                        out=y[:],
+                        lhsT=w_codes[:, t, :].bitcast(FP8X4),
+                        lhsT_scale=w_scales[:, t, :],
+                        rhs=h_codes[:, columns].bitcast(FP8X4),
+                        rhs_scale=h_scales[:, columns],
+                        start=True,
+                        stop=True,
+                    )
+                    live["y", c, t] = y
 
-        def leave_psum(c):
-            q_rows = work.tile([P, PACK, CHUNK], BF16)
-            for t in range(PACK):
-                nc.scalar.activation(
-                    out=q_rows[:, t, :],
-                    in_=live.pop(("y", c, t))[:],
-                    func=ACT.Relu,
-                    bias=shift[:, t : t + 1],
-                    scale=gain[:, t : t + 1],
-                )
-            live["q_rows", c] = q_rows
+        def leave_psum(g):
+            chunks = GROUPS[g]
+            q_rows = work.tile([P, PACK, len(chunks) * CHUNK], BF16)
+            for k, c in enumerate(chunks):
+                for t in range(PACK):
+                    nc.scalar.activation(
+                        out=q_rows[:, t, k * CHUNK : (k + 1) * CHUNK],
+                        in_=live.pop(("y", c, t))[:],
+                        func=ACT.Relu,
+                        bias=shift[:, t : t + 1],
+                        scale=gain[:, t : t + 1],
+                    )
+            live["q_rows", g] = q_rows
 
-        def q_regroup(c):
-            q_grouped = work.tile([P, CHUNK, PACK], BF16, align_bytes=64)
-            regroup(nc, q_grouped[:], live.pop(("q_rows", c))[:])
-            live["q_grouped", c] = q_grouped
+        def q_regroup(g):
+            q_grouped = work.tile([P, len(GROUPS[g]) * CHUNK, PACK], BF16, align_bytes=64)
+            regroup(nc, q_grouped[:], live.pop(("q_rows", g))[:])
+            live["q_grouped", g] = q_grouped
 
-        def q_quantise(c):
-            q_codes = work.tile([P, CHUNK], U32, align_bytes=64)
-            q_scales = work.tile([P, CHUNK], U8, align_bytes=64)
+        def q_quantise(g):
+            width = len(GROUPS[g]) * CHUNK
+            q_codes = work.tile([P, width], U32, align_bytes=64)
+            q_scales = work.tile([P, width], U8, align_bytes=64)
             nc.vector.quantize_mx(
                 out=q_codes[:].bitcast(FP8X4),
                 scales=q_scales[:],
-                in_=live.pop(("q_grouped", c))[:].rearrange("p w j -> p (w j)"),
+                in_=live.pop(("q_grouped", g))[:].rearrange("p w j -> p (w j)"),
             )
-            live["q_mx", c] = (q_codes, q_scales)
+            live["q_mx", g] = (q_codes, q_scales)
 
-        def key_quantise(n):
-            key_grouped = work.tile([P, REGIONS, PACK], BF16, align_bytes=64)
-            regroup(nc, key_grouped[:], key_rows[:, n, :, :])
-            key_codes = work.tile([P, REGIONS], U32, align_bytes=64)
-            key_scales = work.tile([P, REGIONS], U8, align_bytes=64)
+        def key_regroup():
+            key_grouped = keep.tile([P, IMAGES * REGIONS, PACK], BF16, align_bytes=64)
+            regroup(nc, key_grouped[:], key_rows[:].rearrange("p j n m -> p j (n m)"))
+            live["key_grouped"] = key_grouped
+
+        def key_quantise():
+            key_codes = keep.tile([P, IMAGES * REGIONS], U32, align_bytes=64)
+            key_scales = keep.tile([P, IMAGES * REGIONS], U8, align_bytes=64)
             nc.vector.quantize_mx(
                 out=key_codes[:].bitcast(FP8X4),
                 scales=key_scales[:],
-                in_=key_grouped[:].rearrange("p m j -> p (m j)"),
+                in_=live.pop("key_grouped")[:].rearrange("p m j -> p (m j)"),
             )
             live["key_mx"] = (key_codes, key_scales)
 
-        def scores(c):
-            if c % CHUNKS_PER_IMAGE == 0:
-                key_quantise(c // CHUNKS_PER_IMAGE)
+        def scores(g):
             key_codes, key_scales = live["key_mx"]
-            q_codes, q_scales = live.pop(("q_mx", c))
-            sim = sim_banks.tile([P, TILES, REGIONS], F32, tag="sim")
-            for i in range(TILES):
-                nc.tensor.matmul_mx(
-                    out=sim[:, i, :],
-                    lhsT=q_codes[:, i * P : (i + 1) * P].bitcast(FP8X4),
-                    lhsT_scale=q_scales[:, i * P : (i + 1) * P],
-                    rhs=key_codes[:].bitcast(FP8X4),
-                    rhs_scale=key_scales[:],
-                    start=True,
-                    stop=True,
+            q_codes, q_scales = live.pop(("q_mx", g))
+            for k, c in enumerate(GROUPS[g]):
+                n = c // CHUNKS_PER_IMAGE
+                regions = slice(n * REGIONS, (n + 1) * REGIONS)
+                sim = sim_banks.tile([P, TILES, REGIONS], F32, tag="sim")
+                for i in range(TILES):
+                    pixels = slice((k * TILES + i) * P, (k * TILES + i + 1) * P)
+                    nc.tensor.matmul_mx(
+                        out=sim[:, i, :],
+                        lhsT=q_codes[:, pixels].bitcast(FP8X4),
+                        lhsT_scale=q_scales[:, pixels],
+                        rhs=key_codes[:, regions].bitcast(FP8X4),
+                        rhs_scale=key_scales[:, regions],
+                        start=True,
+                        stop=True,
+                    )
+                live["sim", c] = sim
+
+        def row_max(g):
+            chunks = GROUPS[g]
+            top = small.tile([P, len(chunks) * TILES], F32)
+            for k, c in enumerate(chunks):
+                nc.vector.tensor_reduce(
+                    out=top[:, k * TILES : (k + 1) * TILES], in_=live["sim", c][:], axis=AXIS.X, op=ALU.max
                 )
-            live["sim", c] = sim
+            live["top", g] = top
 
-        def row_max(c):
-            top = small.tile([P, TILES], F32)
-            nc.vector.tensor_reduce(out=top[:], in_=live["sim", c][:], axis=AXIS.X, op=ALU.max)
-            live["top", c] = top
-
-        def row_shift(c):
-            minus_top = small.tile([P, TILES], F32)
-            nc.vector.tensor_scalar_mul(out=minus_top[:], in0=live.pop(("top", c))[:], scalar1=-SIM_SCALE)
-            live["minus_top", c] = minus_top
-
-        def exponent(c):
-            sim = live.pop(("sim", c))
-            minus_top = live.pop(("minus_top", c))
-            e = result.tile([P, TILES, REGIONS], F32)
-            sums = small.tile([P, TILES], F32)
-            for i in range(TILES):
-                nc.scalar.activation(
-                    out=e[:, i, :],
-                    in_=sim[:, i, :],
-                    func=ACT.Exp,
-                    bias=minus_top[:, i : i + 1],
-                    scale=SIM_SCALE,
-                    accum_out=sums[:, i : i + 1],
-                )
-            live["e", c] = e
-            live["sums", c] = sums
-
-        def invert_sums(c):
-            inverse = small.tile([P, TILES], F32)
-            nc.vector.reciprocal(out=inverse[:], in_=live.pop(("sums", c))[:])
-            live["inverse", c] = inverse
-
-        def normalise(c):
-            n, first = divmod(c * CHUNK, PIXELS)
-            e = live.pop(("e", c))
-            inverse = live.pop(("inverse", c))
-            for i in range(TILES):
-                nc.scalar.activation(out=e[:, i, :], in_=e[:, i, :], func=ACT.Copy, scale=inverse[:, i : i + 1])
-            nc.sync.dma_start(
-                out=out[n, first : first + CHUNK, :].rearrange("(i p) m -> p i m", p=P), in_=e[:]
+        def row_shift(g):
+            minus_top = small.tile([P, len(GROUPS[g]) * TILES], F32)
+            nc.gpsimd.tensor_scalar(
+                out=minus_top[:], in0=live.pop(("top", g))[:], scalar1=-SIM_SCALE, scalar2=None, op0=ALU.mult
             )
+            live["minus_top", g] = minus_top
 
-        def at(stage, c):
-            if 0 <= c < CHUNKS:
-                stage(c)
+        def exponent(g):
+            chunks = GROUPS[g]
+            minus_top = live.pop(("minus_top", g))
+            e = result.tile([P, len(chunks) * TILES, REGIONS], F32)
+            sums = small.tile([P, len(chunks) * TILES], F32)
+            for k, c in enumerate(chunks):
+                sim = live.pop(("sim", c))
+                for i in range(TILES):
+                    j = k * TILES + i
+                    nc.scalar.activation(
+                        out=e[:, j, :],
+                        in_=sim[:, i, :],
+                        func=ACT.Exp,
+                        bias=minus_top[:, j : j + 1],
+                        scale=SIM_SCALE,
+                        accum_out=sums[:, j : j + 1],
+                    )
+            live["e", g] = e
+            live["sums", g] = sums
 
-        for c in range(LEAD):
-            load(c)
-        for s in range(CHUNKS + DEPTH):
+        def invert_sums(g):
+            inverse = small.tile([P, len(GROUPS[g]) * TILES], F32)
+            nc.vector.reciprocal(out=inverse[:], in_=live.pop(("sums", g))[:])
+            live["inverse", g] = inverse
+
+        def normalise(g):
+            e = live.pop(("e", g))
+            inverse = live.pop(("inverse", g))
+            chunks = GROUPS[g]
+            for k, c in enumerate(chunks):
+                n, first = divmod(c * CHUNK, PIXELS)
+                for i in range(TILES):
+                    j = k * TILES + i
+                    nc.scalar.activation(out=e[:, j, :], in_=e[:, j, :], func=ACT.Copy, scale=inverse[:, j : j + 1])
+                nc.sync.dma_start(
+                    out=out[n, first : first + CHUNK, :].rearrange("(i p) m -> p i m", p=P),
+                    in_=e[:, k * TILES : (k + 1) * TILES, :],
+                )
+
+        def at(stage, g):
+            if 0 <= g < len(GROUPS):
+                stage(g)
+
+        for g in range(LEAD):
+            load(g)
+        for s in range(len(GROUPS) + DEPTH):
             at(load, s + LEAD)
             at(leave_psum, s - 1)
             at(q_regroup, s - 2)
             at(row_max, s - 3)
-            at(h_regroup, s)
             at(row_shift, s - 3)
+            at(h_regroup, s)
+            if s == 1:
+                key_regroup()
             at(q_quantise, s - 2)
             at(scores, s - 2)
             at(invert_sums, s - 4)
             at(h_quantise, s)
+            if s == 1:
+                key_quantise()
             at(project, s)
             at(normalise, s - DEPTH)
             at(exponent, s - 3)

@@ -23,14 +23,17 @@ TILES = CHUNK // P
 CHUNKS = IMAGES * PIXELS // CHUNK
 CHUNKS_PER_IMAGE = PIXELS // CHUNK
 GROUP = 2
-RUN = 4
+RUN = 8
 SIM_SCALE = CHANNELS ** -0.5
 
 GROUPS = [[0]] + [[c, c + 1] for c in range(1, CHUNKS - 1, GROUP)] + [[CHUNKS - 1]]
 
 LEAD = 4
-DEPTH = 5
+DEPTH = 6
 WORK_BUFS = 3
+QUERY_BUFS = 4
+Q_LAG = 3
+VECTOR_ENDS = 2
 RESULT_BUFS = 4
 SMALL_BUFS = 4
 Y_BANKS = 4
@@ -52,6 +55,7 @@ def tile_spatialocr_module_pa_t_kernel(tc, h_pix, wp2, sp2, bp2, key_obj, out):
         keep = ctx.enter_context(tc.tile_pool(name="keep", bufs=1))
         stream = ctx.enter_context(tc.tile_pool(name="stream", bufs=LEAD + 2))
         work = ctx.enter_context(tc.tile_pool(name="work", bufs=WORK_BUFS))
+        query = ctx.enter_context(tc.tile_pool(name="query", bufs=QUERY_BUFS))
         result = ctx.enter_context(tc.tile_pool(name="result", bufs=RESULT_BUFS))
         small = ctx.enter_context(tc.tile_pool(name="small", bufs=SMALL_BUFS))
         y_banks = ctx.enter_context(tc.psum_pool(name="y_banks", bufs=Y_BANKS))
@@ -112,17 +116,21 @@ def tile_spatialocr_module_pa_t_kernel(tc, h_pix, wp2, sp2, bp2, key_obj, out):
             w_grouped = keep.tile([P, PACK, P * PACK], BF16, align_bytes=64)
             w_codes = keep.tile([P, PACK, P], U32, align_bytes=64)
             w_scales = keep.tile([P, PACK, P], U8, align_bytes=64)
-            for t in range(PACK):
-                w_t = sim_banks.tile([P, 2, P], F32, tag="sim")
-                for u in range(2):
-                    nc.tensor.transpose(w_t[:, u, :], w_words[:, t, u, :], ident[:])
-                nc.vector.tensor_copy(
-                    out=w_grouped[:, t, :].bitcast(F32).rearrange("p (o u) -> p o u", u=2),
-                    in_=w_t[:].rearrange("p u o -> p o u"),
-                )
-                nc.vector.quantize_mx(
-                    out=w_codes[:, t, :].bitcast(FP8X4), scales=w_scales[:, t, :], in_=w_grouped[:, t, :]
-                )
+            for t in range(PACK + 1):
+                if t < PACK:
+                    w_t = sim_banks.tile([P, 2, P], F32, tag="sim")
+                    for u in range(2):
+                        nc.tensor.transpose(w_t[:, u, :], w_words[:, t, u, :], ident[:])
+                    nc.vector.tensor_copy(
+                        out=w_grouped[:, t, :].bitcast(F32).rearrange("p (o u) -> p o u", u=2),
+                        in_=w_t[:].rearrange("p u o -> p o u"),
+                    )
+                if t > 0:
+                    nc.vector.quantize_mx(
+                        out=w_codes[:, t - 1, :].bitcast(FP8X4),
+                        scales=w_scales[:, t - 1, :],
+                        in_=w_grouped[:, t - 1, :],
+                    )
             live["w_mx"] = (w_codes, w_scales)
 
         def project(g):
@@ -147,7 +155,7 @@ def tile_spatialocr_module_pa_t_kernel(tc, h_pix, wp2, sp2, bp2, key_obj, out):
 
         def leave_psum(g):
             chunks = GROUPS[g]
-            q_rows = work.tile([P, PACK, len(chunks) * CHUNK], BF16)
+            q_rows = query.tile([P, PACK, len(chunks) * CHUNK], BF16)
             for k, c in enumerate(chunks):
                 for t in range(PACK):
                     nc.scalar.activation(
@@ -221,9 +229,7 @@ def tile_spatialocr_module_pa_t_kernel(tc, h_pix, wp2, sp2, bp2, key_obj, out):
 
         def row_shift(g):
             minus_top = small.tile([P, len(GROUPS[g]) * TILES], F32)
-            nc.gpsimd.tensor_scalar(
-                out=minus_top[:], in0=live.pop(("top", g))[:], scalar1=-SIM_SCALE, scalar2=None, op0=ALU.mult
-            )
+            nc.scalar.activation(out=minus_top[:], in_=live.pop(("top", g))[:], func=ACT.Copy, scale=-SIM_SCALE)
             live["minus_top", g] = minus_top
 
         def exponent(g):
@@ -259,7 +265,10 @@ def tile_spatialocr_module_pa_t_kernel(tc, h_pix, wp2, sp2, bp2, key_obj, out):
                 n, first = divmod(c * CHUNK, PIXELS)
                 for i in range(TILES):
                     j = k * TILES + i
-                    nc.scalar.activation(out=e[:, j, :], in_=e[:, j, :], func=ACT.Copy, scale=inverse[:, j : j + 1])
+                    if g < len(GROUPS) - VECTOR_ENDS:
+                        nc.scalar.activation(out=e[:, j, :], in_=e[:, j, :], func=ACT.Copy, scale=inverse[:, j : j + 1])
+                    else:
+                        nc.vector.tensor_scalar_mul(out=e[:, j, :], in0=e[:, j, :], scalar1=inverse[:, j : j + 1])
                 nc.sync.dma_start(
                     out=out[n, first : first + CHUNK, :].rearrange("(i p) m -> p i m", p=P),
                     in_=e[:, k * TILES : (k + 1) * TILES, :],
@@ -274,18 +283,18 @@ def tile_spatialocr_module_pa_t_kernel(tc, h_pix, wp2, sp2, bp2, key_obj, out):
         for s in range(len(GROUPS) + DEPTH):
             at(load, s + LEAD)
             at(leave_psum, s - 1)
-            at(q_regroup, s - 2)
-            at(row_max, s - 3)
-            at(row_shift, s - 3)
+            at(q_regroup, s - Q_LAG)
+            at(row_max, s - Q_LAG - 1)
             at(h_regroup, s)
-            if s == 1:
+            if s == 2:
                 key_regroup()
-            at(q_quantise, s - 2)
-            at(scores, s - 2)
-            at(invert_sums, s - 4)
+            at(q_quantise, s - Q_LAG)
+            at(scores, s - Q_LAG)
+            at(invert_sums, s - Q_LAG - 2)
             at(h_quantise, s)
-            if s == 1:
+            if s == 2:
                 key_quantise()
             at(project, s)
-            at(normalise, s - DEPTH)
-            at(exponent, s - 3)
+            at(row_shift, s - Q_LAG - 1)
+            at(exponent, s - Q_LAG - 1)
+            at(normalise, s - Q_LAG - 2)

@@ -34,6 +34,7 @@ WORK_BUFS = 3
 QUERY_BUFS = 4
 Q_LAG = 3
 VECTOR_ENDS = 2
+SHARE = 64
 RESULT_BUFS = 4
 SMALL_BUFS = 4
 Y_BANKS = 4
@@ -42,8 +43,8 @@ SIM_BANKS = 4
 FLOPS = 2 * IMAGES * PIXELS * CHANNELS * (CHANNELS + REGIONS)
 
 
-def regroup(nc, grouped, rows):
-    nc.vector.tensor_copy(
+def regroup(copy, grouped, rows):
+    copy(
         out=grouped.rearrange("p (c i) j -> p c j i", i=RUN),
         in_=rows.rearrange("p j (c i) -> p c j i", i=RUN),
     )
@@ -55,6 +56,7 @@ def tile_spatialocr_module_pa_t_kernel(tc, h_pix, wp2, sp2, bp2, key_obj, out):
         keep = ctx.enter_context(tc.tile_pool(name="keep", bufs=1))
         stream = ctx.enter_context(tc.tile_pool(name="stream", bufs=LEAD + 2))
         work = ctx.enter_context(tc.tile_pool(name="work", bufs=WORK_BUFS))
+        grouped = ctx.enter_context(tc.tile_pool(name="grouped", bufs=WORK_BUFS + 1))
         query = ctx.enter_context(tc.tile_pool(name="query", bufs=QUERY_BUFS))
         result = ctx.enter_context(tc.tile_pool(name="result", bufs=RESULT_BUFS))
         small = ctx.enter_context(tc.tile_pool(name="small", bufs=SMALL_BUFS))
@@ -95,10 +97,16 @@ def tile_spatialocr_module_pa_t_kernel(tc, h_pix, wp2, sp2, bp2, key_obj, out):
                 )
             live["h_rows", g] = h_rows
 
-        def h_regroup(g):
-            h_grouped = work.tile([P, len(GROUPS[g]) * CHUNK, PACK], BF16, align_bytes=64)
-            regroup(nc, h_grouped[:], live.pop(("h_rows", g))[:])
+        def h_regroup_scalar(g):
+            h_grouped = grouped.tile([P, len(GROUPS[g]) * CHUNK, PACK], BF16, align_bytes=64)
+            share = len(GROUPS[g]) * SHARE
+            if share:
+                regroup(nc.scalar.copy, h_grouped[:, :share, :], live["h_rows", g][:, :, :share])
             live["h_grouped", g] = h_grouped
+
+        def h_regroup(g):
+            share = len(GROUPS[g]) * SHARE
+            regroup(nc.vector.tensor_copy, live["h_grouped", g][:, share:, :], live.pop(("h_rows", g))[:, :, share:])
 
         def h_quantise(g):
             width = len(GROUPS[g]) * CHUNK
@@ -169,7 +177,7 @@ def tile_spatialocr_module_pa_t_kernel(tc, h_pix, wp2, sp2, bp2, key_obj, out):
 
         def q_regroup(g):
             q_grouped = work.tile([P, len(GROUPS[g]) * CHUNK, PACK], BF16, align_bytes=64)
-            regroup(nc, q_grouped[:], live.pop(("q_rows", g))[:])
+            regroup(nc.vector.tensor_copy, q_grouped[:], live.pop(("q_rows", g))[:])
             live["q_grouped", g] = q_grouped
 
         def q_quantise(g):
@@ -185,7 +193,7 @@ def tile_spatialocr_module_pa_t_kernel(tc, h_pix, wp2, sp2, bp2, key_obj, out):
 
         def key_regroup():
             key_grouped = keep.tile([P, IMAGES * REGIONS, PACK], BF16, align_bytes=64)
-            regroup(nc, key_grouped[:], key_rows[:].rearrange("p j n m -> p j (n m)"))
+            regroup(nc.vector.tensor_copy, key_grouped[:], key_rows[:].rearrange("p j n m -> p j (n m)"))
             live["key_grouped"] = key_grouped
 
         def key_quantise():
@@ -280,6 +288,7 @@ def tile_spatialocr_module_pa_t_kernel(tc, h_pix, wp2, sp2, bp2, key_obj, out):
 
         for g in range(LEAD):
             load(g)
+        h_regroup_scalar(0)
         for s in range(len(GROUPS) + DEPTH):
             at(load, s + LEAD)
             at(leave_psum, s - 1)
@@ -298,3 +307,4 @@ def tile_spatialocr_module_pa_t_kernel(tc, h_pix, wp2, sp2, bp2, key_obj, out):
             at(row_shift, s - Q_LAG - 1)
             at(exponent, s - Q_LAG - 1)
             at(normalise, s - Q_LAG - 2)
+            at(h_regroup_scalar, s + 1)

@@ -18,29 +18,33 @@ IMAGES = 4
 CHANNELS = P * PACK
 PIXELS = 4096
 REGIONS = 128
-CHUNK = 512
-TILES = CHUNK // P
-CHUNKS = IMAGES * PIXELS // CHUNK
-CHUNKS_PER_IMAGE = PIXELS // CHUNK
-GROUP = 2
-RUN = 8
 SIM_SCALE = CHANNELS ** -0.5
+BANK = 512
 
-GROUPS = [[0]] + [[c, c + 1] for c in range(1, CHUNKS - 1, GROUP)] + [[CHUNKS - 1]]
+COLUMNS = IMAGES * PIXELS
+GROUP = 1024
+FIRST = [512]
+LAST = [512]
+WIDTHS = FIRST + [GROUP] * ((COLUMNS - sum(FIRST) - sum(LAST)) // GROUP) + LAST
+STARTS = [sum(WIDTHS[:g]) for g in range(len(WIDTHS))]
 
-LEAD = 4
-DEPTH = 6
-WORK_BUFS = 3
-QUERY_BUFS = 4
+RUN = 8
+SHARE = 8
+NOSHARE = 4
+SHARES = [w // SHARE if g < len(WIDTHS) - NOSHARE else 0 for g, w in enumerate(WIDTHS)]
+LEAD = 5
 Q_LAG = 3
-VECTOR_ENDS = 2
-SHARE = 64
+DEPTH = 6
+VECTOR_ENDS = 3
+WORK_BUFS = 3
+GROUPED_BUFS = 4
+QUERY_BUFS = 4
 RESULT_BUFS = 4
 SMALL_BUFS = 4
 Y_BANKS = 4
 SIM_BANKS = 4
 
-FLOPS = 2 * IMAGES * PIXELS * CHANNELS * (CHANNELS + REGIONS)
+FLOPS = 2 * COLUMNS * CHANNELS * (CHANNELS + REGIONS)
 
 
 def regroup(copy, grouped, rows):
@@ -50,13 +54,24 @@ def regroup(copy, grouped, rows):
     )
 
 
+def pieces(g, width):
+    cut = []
+    done = 0
+    while done < WIDTHS[g]:
+        n, pixel = divmod(STARTS[g] + done, PIXELS)
+        w = min(width, WIDTHS[g] - done, PIXELS - pixel)
+        cut.append((n, pixel, done, w))
+        done += w
+    return cut
+
+
 def tile_spatialocr_module_pa_t_kernel(tc, h_pix, wp2, sp2, bp2, key_obj, out):
     nc = tc.nc
     with ExitStack() as ctx:
         keep = ctx.enter_context(tc.tile_pool(name="keep", bufs=1))
         stream = ctx.enter_context(tc.tile_pool(name="stream", bufs=LEAD + 2))
         work = ctx.enter_context(tc.tile_pool(name="work", bufs=WORK_BUFS))
-        grouped = ctx.enter_context(tc.tile_pool(name="grouped", bufs=WORK_BUFS + 1))
+        grouped = ctx.enter_context(tc.tile_pool(name="grouped", bufs=GROUPED_BUFS))
         query = ctx.enter_context(tc.tile_pool(name="query", bufs=QUERY_BUFS))
         result = ctx.enter_context(tc.tile_pool(name="result", bufs=RESULT_BUFS))
         small = ctx.enter_context(tc.tile_pool(name="small", bufs=SMALL_BUFS))
@@ -64,15 +79,32 @@ def tile_spatialocr_module_pa_t_kernel(tc, h_pix, wp2, sp2, bp2, key_obj, out):
         sim_banks = ctx.enter_context(tc.psum_pool(name="sim_banks", bufs=SIM_BANKS))
         ctx.enter_context(tc.manual_schedule())
 
-        w_rows = keep.tile([P, PACK * CHANNELS], BF16)
-        nc.scalar.dma_start(out=w_rows[:], in_=wp2.rearrange("(p t) k -> p (t k)", t=PACK))
+        live = {}
+
+        def load(g):
+            h_rows = stream.tile([P, PACK, WIDTHS[g]], BF16)
+            for n, pixel, column, w in pieces(g, GROUP):
+                nc.sync.dma_start(
+                    out=h_rows[:, :, column : column + w],
+                    in_=h_pix[n, :, pixel : pixel + w].rearrange("(p j) w -> p j w", j=PACK),
+                )
+            live["h_rows", g] = h_rows
+
         gain_bf = keep.tile([P, PACK], BF16)
         nc.scalar.dma_start(out=gain_bf[:], in_=sp2.rearrange("(p t) -> p t", t=PACK))
         shift_bf = keep.tile([P, PACK], BF16)
         nc.scalar.dma_start(out=shift_bf[:], in_=bp2.rearrange("(p t) -> p t", t=PACK))
+        load(0)
+        w_rows = keep.tile([P, PACK, CHANNELS], BF16)
+        w_source = wp2.rearrange("(p t) k -> p t k", t=PACK)
+        for t in range(PACK):
+            nc.sync.dma_start(out=w_rows[:, t, :], in_=w_source[:, t, :])
         key_rows = keep.tile([P, PACK, IMAGES, REGIONS], BF16)
-        for n in range(IMAGES):
-            nc.scalar.dma_start(out=key_rows[:, :, n, :], in_=key_obj[n].rearrange("(p j) m -> p j m", j=PACK))
+        for g in range(1, LEAD):
+            load(g)
+            if g == Q_LAG - 1:
+                for n in range(IMAGES):
+                    nc.sync.dma_start(out=key_rows[:, :, n, :], in_=key_obj[n].rearrange("(p j) m -> p j m", j=PACK))
 
         ident = keep.tile([P, P], F32)
         make_identity(nc, ident[:])
@@ -81,37 +113,20 @@ def tile_spatialocr_module_pa_t_kernel(tc, h_pix, wp2, sp2, bp2, key_obj, out):
         shift = keep.tile([P, PACK], F32)
         nc.gpsimd.tensor_copy(out=shift[:], in_=shift_bf[:])
 
-        live = {}
-
-        def load(g):
-            chunks = GROUPS[g]
-            h_rows = stream.tile([P, PACK, len(chunks) * CHUNK], BF16)
-            for n in sorted({c // CHUNKS_PER_IMAGE for c in chunks}):
-                mine = [c for c in chunks if c // CHUNKS_PER_IMAGE == n]
-                first = mine[0] % CHUNKS_PER_IMAGE * CHUNK
-                at_column = (mine[0] - chunks[0]) * CHUNK
-                width = len(mine) * CHUNK
-                nc.sync.dma_start(
-                    out=h_rows[:, :, at_column : at_column + width],
-                    in_=h_pix[n, :, first : first + width].rearrange("(p j) w -> p j w", j=PACK),
-                )
-            live["h_rows", g] = h_rows
-
         def h_regroup_scalar(g):
-            h_grouped = grouped.tile([P, len(GROUPS[g]) * CHUNK, PACK], BF16, align_bytes=64)
-            share = len(GROUPS[g]) * SHARE
+            h_grouped = grouped.tile([P, WIDTHS[g], PACK], BF16, align_bytes=64)
+            share = SHARES[g]
             if share:
                 regroup(nc.scalar.copy, h_grouped[:, :share, :], live["h_rows", g][:, :, :share])
             live["h_grouped", g] = h_grouped
 
         def h_regroup(g):
-            share = len(GROUPS[g]) * SHARE
+            share = SHARES[g]
             regroup(nc.vector.tensor_copy, live["h_grouped", g][:, share:, :], live.pop(("h_rows", g))[:, :, share:])
 
         def h_quantise(g):
-            width = len(GROUPS[g]) * CHUNK
-            h_codes = work.tile([P, width], U32, align_bytes=64)
-            h_scales = work.tile([P, width], U8, align_bytes=64)
+            h_codes = work.tile([P, WIDTHS[g]], U32, align_bytes=64)
+            h_scales = work.tile([P, WIDTHS[g]], U8, align_bytes=64)
             nc.vector.quantize_mx(
                 out=h_codes[:].bitcast(FP8X4),
                 scales=h_scales[:],
@@ -120,7 +135,7 @@ def tile_spatialocr_module_pa_t_kernel(tc, h_pix, wp2, sp2, bp2, key_obj, out):
             live["h_mx", g] = (h_codes, h_scales)
 
         def w_quantise():
-            w_words = w_rows[:].bitcast(F32).rearrange("p (t q u) -> p t u q", t=PACK, u=2)
+            w_words = w_rows[:].rearrange("p t k -> p (t k)").bitcast(F32).rearrange("p (t q u) -> p t u q", t=PACK, u=2)
             w_grouped = keep.tile([P, PACK, P * PACK], BF16, align_bytes=64)
             w_codes = keep.tile([P, PACK, P], U32, align_bytes=64)
             w_scales = keep.tile([P, PACK, P], U8, align_bytes=64)
@@ -146,29 +161,29 @@ def tile_spatialocr_module_pa_t_kernel(tc, h_pix, wp2, sp2, bp2, key_obj, out):
                 w_quantise()
             w_codes, w_scales = live["w_mx"]
             h_codes, h_scales = live.pop(("h_mx", g))
-            for k, c in enumerate(GROUPS[g]):
-                columns = slice(k * CHUNK, (k + 1) * CHUNK)
+            for column in range(0, WIDTHS[g], BANK):
+                w = min(BANK, WIDTHS[g] - column)
                 for t in range(PACK):
-                    y = y_banks.tile([P, CHUNK], F32)
+                    y = y_banks.tile([P, BANK], F32)
                     nc.tensor.matmul_mx(
-                        out=y[:],
+                        out=y[:, :w],
                         lhsT=w_codes[:, t, :].bitcast(FP8X4),
                         lhsT_scale=w_scales[:, t, :],
-                        rhs=h_codes[:, columns].bitcast(FP8X4),
-                        rhs_scale=h_scales[:, columns],
+                        rhs=h_codes[:, column : column + w].bitcast(FP8X4),
+                        rhs_scale=h_scales[:, column : column + w],
                         start=True,
                         stop=True,
                     )
-                    live["y", c, t] = y
+                    live["y", g, column, t] = y
 
         def leave_psum(g):
-            chunks = GROUPS[g]
-            q_rows = query.tile([P, PACK, len(chunks) * CHUNK], BF16)
-            for k, c in enumerate(chunks):
+            q_rows = query.tile([P, PACK, WIDTHS[g]], BF16)
+            for column in range(0, WIDTHS[g], BANK):
+                w = min(BANK, WIDTHS[g] - column)
                 for t in range(PACK):
                     nc.scalar.activation(
-                        out=q_rows[:, t, k * CHUNK : (k + 1) * CHUNK],
-                        in_=live.pop(("y", c, t))[:],
+                        out=q_rows[:, t, column : column + w],
+                        in_=live.pop(("y", g, column, t))[:, :w],
                         func=ACT.Relu,
                         bias=shift[:, t : t + 1],
                         scale=gain[:, t : t + 1],
@@ -176,14 +191,13 @@ def tile_spatialocr_module_pa_t_kernel(tc, h_pix, wp2, sp2, bp2, key_obj, out):
             live["q_rows", g] = q_rows
 
         def q_regroup(g):
-            q_grouped = work.tile([P, len(GROUPS[g]) * CHUNK, PACK], BF16, align_bytes=64)
+            q_grouped = work.tile([P, WIDTHS[g], PACK], BF16, align_bytes=64)
             regroup(nc.vector.tensor_copy, q_grouped[:], live.pop(("q_rows", g))[:])
             live["q_grouped", g] = q_grouped
 
         def q_quantise(g):
-            width = len(GROUPS[g]) * CHUNK
-            q_codes = work.tile([P, width], U32, align_bytes=64)
-            q_scales = work.tile([P, width], U8, align_bytes=64)
+            q_codes = work.tile([P, WIDTHS[g]], U32, align_bytes=64)
+            q_scales = work.tile([P, WIDTHS[g]], U8, align_bytes=64)
             nc.vector.quantize_mx(
                 out=q_codes[:].bitcast(FP8X4),
                 scales=q_scales[:],
@@ -209,46 +223,48 @@ def tile_spatialocr_module_pa_t_kernel(tc, h_pix, wp2, sp2, bp2, key_obj, out):
         def scores(g):
             key_codes, key_scales = live["key_mx"]
             q_codes, q_scales = live.pop(("q_mx", g))
-            for k, c in enumerate(GROUPS[g]):
-                n = c // CHUNKS_PER_IMAGE
-                regions = slice(n * REGIONS, (n + 1) * REGIONS)
-                sim = sim_banks.tile([P, TILES, REGIONS], F32, tag="sim")
-                for i in range(TILES):
-                    pixels = slice((k * TILES + i) * P, (k * TILES + i + 1) * P)
+            for column in range(0, WIDTHS[g], BANK):
+                w = min(BANK, WIDTHS[g] - column)
+                sim = sim_banks.tile([P, BANK // P, REGIONS], F32, tag="sim")
+                for i in range(w // P):
+                    first = column + i * P
+                    n = (STARTS[g] + first) // PIXELS
                     nc.tensor.matmul_mx(
                         out=sim[:, i, :],
-                        lhsT=q_codes[:, pixels].bitcast(FP8X4),
-                        lhsT_scale=q_scales[:, pixels],
-                        rhs=key_codes[:, regions].bitcast(FP8X4),
-                        rhs_scale=key_scales[:, regions],
+                        lhsT=q_codes[:, first : first + P].bitcast(FP8X4),
+                        lhsT_scale=q_scales[:, first : first + P],
+                        rhs=key_codes[:, n * REGIONS : (n + 1) * REGIONS].bitcast(FP8X4),
+                        rhs_scale=key_scales[:, n * REGIONS : (n + 1) * REGIONS],
                         start=True,
                         stop=True,
                     )
-                live["sim", c] = sim
+                live["sim", g, column] = sim
 
         def row_max(g):
-            chunks = GROUPS[g]
-            top = small.tile([P, len(chunks) * TILES], F32)
-            for k, c in enumerate(chunks):
+            top = small.tile([P, WIDTHS[g] // P], F32)
+            for column in range(0, WIDTHS[g], BANK):
+                w = min(BANK, WIDTHS[g] - column)
                 nc.vector.tensor_reduce(
-                    out=top[:, k * TILES : (k + 1) * TILES], in_=live["sim", c][:], axis=AXIS.X, op=ALU.max
+                    out=top[:, column // P : (column + w) // P],
+                    in_=live["sim", g, column][:, : w // P, :],
+                    axis=AXIS.X,
+                    op=ALU.max,
                 )
             live["top", g] = top
 
         def row_shift(g):
-            minus_top = small.tile([P, len(GROUPS[g]) * TILES], F32)
+            minus_top = small.tile([P, WIDTHS[g] // P], F32)
             nc.scalar.activation(out=minus_top[:], in_=live.pop(("top", g))[:], func=ACT.Copy, scale=-SIM_SCALE)
             live["minus_top", g] = minus_top
 
         def exponent(g):
-            chunks = GROUPS[g]
             minus_top = live.pop(("minus_top", g))
-            e = result.tile([P, len(chunks) * TILES, REGIONS], F32)
-            sums = small.tile([P, len(chunks) * TILES], F32)
-            for k, c in enumerate(chunks):
-                sim = live.pop(("sim", c))
-                for i in range(TILES):
-                    j = k * TILES + i
+            e = result.tile([P, WIDTHS[g] // P, REGIONS], F32)
+            sums = small.tile([P, WIDTHS[g] // P], F32)
+            for column in range(0, WIDTHS[g], BANK):
+                sim = live.pop(("sim", g, column))
+                for i in range(min(BANK, WIDTHS[g] - column) // P):
+                    j = column // P + i
                     nc.scalar.activation(
                         out=e[:, j, :],
                         in_=sim[:, i, :],
@@ -261,47 +277,43 @@ def tile_spatialocr_module_pa_t_kernel(tc, h_pix, wp2, sp2, bp2, key_obj, out):
             live["sums", g] = sums
 
         def invert_sums(g):
-            inverse = small.tile([P, len(GROUPS[g]) * TILES], F32)
+            inverse = small.tile([P, WIDTHS[g] // P], F32)
             nc.vector.reciprocal(out=inverse[:], in_=live.pop(("sums", g))[:])
             live["inverse", g] = inverse
 
         def normalise(g):
             e = live.pop(("e", g))
             inverse = live.pop(("inverse", g))
-            chunks = GROUPS[g]
-            for k, c in enumerate(chunks):
-                n, first = divmod(c * CHUNK, PIXELS)
-                for i in range(TILES):
-                    j = k * TILES + i
-                    if g < len(GROUPS) - VECTOR_ENDS:
-                        nc.scalar.activation(out=e[:, j, :], in_=e[:, j, :], func=ACT.Copy, scale=inverse[:, j : j + 1])
-                    else:
-                        nc.vector.tensor_scalar_mul(out=e[:, j, :], in0=e[:, j, :], scalar1=inverse[:, j : j + 1])
+            tiles = WIDTHS[g] // P
+            for j in range(tiles):
+                if g >= len(WIDTHS) - VECTOR_ENDS:
+                    nc.vector.tensor_scalar_mul(out=e[:, j, :], in0=e[:, j, :], scalar1=inverse[:, j : j + 1])
+                else:
+                    nc.scalar.activation(out=e[:, j, :], in_=e[:, j, :], func=ACT.Copy, scale=inverse[:, j : j + 1])
+            for n, pixel, column, w in pieces(g, BANK):
                 nc.sync.dma_start(
-                    out=out[n, first : first + CHUNK, :].rearrange("(i p) m -> p i m", p=P),
-                    in_=e[:, k * TILES : (k + 1) * TILES, :],
+                    out=out[n, pixel : pixel + w, :].rearrange("(i p) m -> p i m", p=P),
+                    in_=e[:, column // P : (column + w) // P, :],
                 )
 
         def at(stage, g):
-            if 0 <= g < len(GROUPS):
+            if 0 <= g < len(WIDTHS):
                 stage(g)
 
-        for g in range(LEAD):
-            load(g)
         h_regroup_scalar(0)
-        for s in range(len(GROUPS) + DEPTH):
+        for s in range(len(WIDTHS) + DEPTH):
             at(load, s + LEAD)
             at(leave_psum, s - 1)
             at(q_regroup, s - Q_LAG)
             at(row_max, s - Q_LAG - 1)
             at(h_regroup, s)
-            if s == 2:
+            if s == Q_LAG - 1:
                 key_regroup()
             at(q_quantise, s - Q_LAG)
             at(scores, s - Q_LAG)
             at(invert_sums, s - Q_LAG - 2)
             at(h_quantise, s)
-            if s == 2:
+            if s == Q_LAG - 1:
                 key_quantise()
             at(project, s)
             at(row_shift, s - Q_LAG - 1)

@@ -25,19 +25,29 @@ COLUMNS = IMAGES * PIXELS
 GROUP = 1024
 FIRST = [512]
 LAST = [512]
-WIDTHS = FIRST + [GROUP] * ((COLUMNS - sum(FIRST) - sum(LAST)) // GROUP) + LAST
+MIDDLE = (COLUMNS - sum(FIRST) - sum(LAST)) // GROUP
+WIDTHS = FIRST + [GROUP] * MIDDLE + LAST
+STEPS = [list(range(len(FIRST)))] + [[len(FIRST) + m] for m in range(MIDDLE)] + [list(range(len(FIRST) + MIDDLE, len(WIDTHS)))]
 STARTS = [sum(WIDTHS[:g]) for g in range(len(WIDTHS))]
 
 RUN = 8
-SHARE = 8
-NOSHARE = 4
-SHARES = [w // SHARE if g < len(WIDTHS) - NOSHARE else 0 for g, w in enumerate(WIDTHS)]
+SHARE = 64
+SFIRST = 1
+SMID = 6
+SEARLY = 192
+NOSHARE = 5
+GSHARE = 128
+GFIRST = 5
+TAILSTEP = len(STEPS)
+GLASTCUT = 1
+GPSIMD_SHARES = [GSHARE if w == GROUP and GFIRST <= g < len(WIDTHS) - GLASTCUT else 0 for g, w in enumerate(WIDTHS)]
+SHARES = [0 if g < SFIRST or g >= len(WIDTHS) - NOSHARE else SEARLY if g < SMID else SHARE for g, w in enumerate(WIDTHS)]
 LEAD = 5
 Q_LAG = 3
-DEPTH = 6
+DEPTH = 7
 VECTOR_ENDS = 3
 WORK_BUFS = 3
-GROUPED_BUFS = 4
+GROUPED_BUFS = 2
 QUERY_BUFS = 4
 RESULT_BUFS = 4
 SMALL_BUFS = 4
@@ -94,15 +104,17 @@ def tile_spatialocr_module_pa_t_kernel(tc, h_pix, wp2, sp2, bp2, key_obj, out):
         nc.scalar.dma_start(out=gain_bf[:], in_=sp2.rearrange("(p t) -> p t", t=PACK))
         shift_bf = keep.tile([P, PACK], BF16)
         nc.scalar.dma_start(out=shift_bf[:], in_=bp2.rearrange("(p t) -> p t", t=PACK))
-        load(0)
+        for g in STEPS[0]:
+            load(g)
         w_rows = keep.tile([P, PACK, CHANNELS], BF16)
         w_source = wp2.rearrange("(p t) k -> p t k", t=PACK)
         for t in range(PACK):
             nc.sync.dma_start(out=w_rows[:, t, :], in_=w_source[:, t, :])
         key_rows = keep.tile([P, PACK, IMAGES, REGIONS], BF16)
-        for g in range(1, LEAD):
-            load(g)
-            if g == Q_LAG - 1:
+        for s in range(1, LEAD):
+            for g in STEPS[s]:
+                load(g)
+            if s == Q_LAG - 1:
                 for n in range(IMAGES):
                     nc.sync.dma_start(out=key_rows[:, :, n, :], in_=key_obj[n].rearrange("(p j) m -> p j m", j=PACK))
 
@@ -113,16 +125,28 @@ def tile_spatialocr_module_pa_t_kernel(tc, h_pix, wp2, sp2, bp2, key_obj, out):
         shift = keep.tile([P, PACK], F32)
         nc.gpsimd.tensor_copy(out=shift[:], in_=shift_bf[:])
 
-        def h_regroup_scalar(g):
+        def h_regroup_gpsimd(g):
             h_grouped = grouped.tile([P, WIDTHS[g], PACK], BF16, align_bytes=64)
-            share = SHARES[g]
+            share = GPSIMD_SHARES[g]
             if share:
-                regroup(nc.scalar.copy, h_grouped[:, :share, :], live["h_rows", g][:, :, :share])
+                nc.gpsimd.tensor_scalar(
+                    out=h_grouped[:, :share, :],
+                    in0=live["h_rows", g][:, :, :share].rearrange("p j w -> p w j"),
+                    scalar1=1.0,
+                    scalar2=0.0,
+                    op0=ALU.mult,
+                    op1=ALU.add,
+                )
             live["h_grouped", g] = h_grouped
 
+        def h_regroup_scalar(g):
+            columns = slice(GPSIMD_SHARES[g], GPSIMD_SHARES[g] + SHARES[g])
+            if SHARES[g]:
+                regroup(nc.scalar.copy, live["h_grouped", g][:, columns, :], live["h_rows", g][:, :, columns])
+
         def h_regroup(g):
-            share = SHARES[g]
-            regroup(nc.vector.tensor_copy, live["h_grouped", g][:, share:, :], live.pop(("h_rows", g))[:, :, share:])
+            rest = slice(GPSIMD_SHARES[g] + SHARES[g], WIDTHS[g])
+            regroup(nc.vector.tensor_copy, live["h_grouped", g][:, rest, :], live.pop(("h_rows", g))[:, :, rest])
 
         def h_quantise(g):
             h_codes = work.tile([P, WIDTHS[g]], U32, align_bytes=64)
@@ -144,7 +168,7 @@ def tile_spatialocr_module_pa_t_kernel(tc, h_pix, wp2, sp2, bp2, key_obj, out):
                     w_t = sim_banks.tile([P, 2, P], F32, tag="sim")
                     for u in range(2):
                         nc.tensor.transpose(w_t[:, u, :], w_words[:, t, u, :], ident[:])
-                    nc.vector.tensor_copy(
+                    nc.scalar.copy(
                         out=w_grouped[:, t, :].bitcast(F32).rearrange("p (o u) -> p o u", u=2),
                         in_=w_t[:].rearrange("p u o -> p o u"),
                     )
@@ -205,10 +229,11 @@ def tile_spatialocr_module_pa_t_kernel(tc, h_pix, wp2, sp2, bp2, key_obj, out):
             )
             live["q_mx", g] = (q_codes, q_scales)
 
+        key_grouped = keep.tile([P, IMAGES * REGIONS, PACK], BF16, align_bytes=64)
+        live["key_grouped"] = key_grouped
+
         def key_regroup():
-            key_grouped = keep.tile([P, IMAGES * REGIONS, PACK], BF16, align_bytes=64)
             regroup(nc.vector.tensor_copy, key_grouped[:], key_rows[:].rearrange("p j n m -> p j (n m)"))
-            live["key_grouped"] = key_grouped
 
         def key_quantise():
             key_codes = keep.tile([P, IMAGES * REGIONS], U32, align_bytes=64)
@@ -296,25 +321,32 @@ def tile_spatialocr_module_pa_t_kernel(tc, h_pix, wp2, sp2, bp2, key_obj, out):
                     in_=e[:, column // P : (column + w) // P, :],
                 )
 
-        def at(stage, g):
-            if 0 <= g < len(WIDTHS):
-                stage(g)
+        def at(stage, s):
+            if 0 <= s < len(STEPS):
+                for g in STEPS[s]:
+                    stage(g)
 
-        h_regroup_scalar(0)
-        for s in range(len(WIDTHS) + DEPTH):
+        for s in range(GROUPED_BUFS):
+            at(h_regroup_gpsimd, s)
+        at(h_regroup_scalar, 0)
+        for s in range(len(STEPS) + DEPTH):
             at(load, s + LEAD)
             at(leave_psum, s - 1)
+            if s < TAILSTEP:
+                at(row_max, s - Q_LAG - 1)
             at(q_regroup, s - Q_LAG)
-            at(row_max, s - Q_LAG - 1)
-            at(h_regroup, s)
+            if s >= TAILSTEP:
+                at(row_max, s - Q_LAG - 1)
             if s == Q_LAG - 1:
                 key_regroup()
+            at(h_regroup, s)
+            if s == Q_LAG:
+                key_quantise()
             at(q_quantise, s - Q_LAG)
             at(scores, s - Q_LAG)
             at(invert_sums, s - Q_LAG - 2)
             at(h_quantise, s)
-            if s == Q_LAG - 1:
-                key_quantise()
+            at(h_regroup_gpsimd, s + GROUPED_BUFS)
             at(project, s)
             at(row_shift, s - Q_LAG - 1)
             at(exponent, s - Q_LAG - 1)

from contextlib import ExitStack

import concourse.mybir as mybir
from concourse.masks import make_identity

F32 = mybir.dt.float32
BF16 = mybir.dt.bfloat16
U32 = mybir.dt.uint32
U8 = mybir.dt.uint8
FP8X4 = mybir.dt.float8_e4m3fn_x4
ACT = mybir.ActivationFunctionType
ALU = mybir.AluOpType
AXIS = mybir.AxisListType

P = 128
PACK = 4
IMAGES = 4
CHANNELS = P * PACK
PIXELS = 4096
REGIONS = 128
SIM_SCALE = CHANNELS ** -0.5
BANK = 512

COLUMNS = IMAGES * PIXELS
GROUP = 1024
FIRST = [512]
LAST = [512]
MIDDLE = (COLUMNS - sum(FIRST) - sum(LAST)) // GROUP
WIDTHS = FIRST + [GROUP] * MIDDLE + LAST
STEPS = [list(range(len(FIRST)))] + [[len(FIRST) + m] for m in range(MIDDLE)] + [list(range(len(FIRST) + MIDDLE, len(WIDTHS)))]
STARTS = [sum(WIDTHS[:g]) for g in range(len(WIDTHS))]

RUN = 8
SHARE = 64
SFIRST = 1
SMID = 6
SEARLY = 192
NOSHARE = 5
GSHARE = 128
GFIRST = 5
TAILSTEP = len(STEPS)
GLASTCUT = 1
GPSIMD_SHARES = [GSHARE if w == GROUP and GFIRST <= g < len(WIDTHS) - GLASTCUT else 0 for g, w in enumerate(WIDTHS)]
SHARES = [0 if g < SFIRST or g >= len(WIDTHS) - NOSHARE else SEARLY if g < SMID else SHARE for g, w in enumerate(WIDTHS)]
LEAD = 5
Q_LAG = 3
DEPTH = 7
VECTOR_ENDS = 3
WORK_BUFS = 3
GROUPED_BUFS = 2
QUERY_BUFS = 4
RESULT_BUFS = 4
SMALL_BUFS = 4
Y_BANKS = 4
SIM_BANKS = 4

FLOPS = 2 * COLUMNS * CHANNELS * (CHANNELS + REGIONS)


def regroup(copy, grouped, rows):
    copy(
        out=grouped.rearrange("p (c i) j -> p c j i", i=RUN),
        in_=rows.rearrange("p j (c i) -> p c j i", i=RUN),
    )


def pieces(g, width):
    cut = []
    done = 0
    while done < WIDTHS[g]:
        n, pixel = divmod(STARTS[g] + done, PIXELS)
        w = min(width, WIDTHS[g] - done, PIXELS - pixel)
        cut.append((n, pixel, done, w))
        done += w
    return cut


def tile_spatialocr_module_pa_t_kernel(tc, h_pix, wp2, sp2, bp2, key_obj, out):
    nc = tc.nc
    with ExitStack() as ctx:
        keep = ctx.enter_context(tc.tile_pool(name="keep", bufs=1))
        stream = ctx.enter_context(tc.tile_pool(name="stream", bufs=LEAD + 2))
        work = ctx.enter_context(tc.tile_pool(name="work", bufs=WORK_BUFS))
        grouped = ctx.enter_context(tc.tile_pool(name="grouped", bufs=GROUPED_BUFS))
        query = ctx.enter_context(tc.tile_pool(name="query", bufs=QUERY_BUFS))
        result = ctx.enter_context(tc.tile_pool(name="result", bufs=RESULT_BUFS))
        small = ctx.enter_context(tc.tile_pool(name="small", bufs=SMALL_BUFS))
        y_banks = ctx.enter_context(tc.psum_pool(name="y_banks", bufs=Y_BANKS))
        sim_banks = ctx.enter_context(tc.psum_pool(name="sim_banks", bufs=SIM_BANKS))
        ctx.enter_context(tc.manual_schedule())

        live = {}

        def load(g):
            h_rows = stream.tile([P, PACK, WIDTHS[g]], BF16)
            for n, pixel, column, w in pieces(g, GROUP):
                nc.sync.dma_start(
                    out=h_rows[:, :, column : column + w],
                    in_=h_pix[n, :, pixel : pixel + w].rearrange("(p j) w -> p j w", j=PACK),
                )
            live["h_rows", g] = h_rows

        gain_bf = keep.tile([P, PACK], BF16)
        nc.scalar.dma_start(out=gain_bf[:], in_=sp2.rearrange("(p t) -> p t", t=PACK))
        shift_bf = keep.tile([P, PACK], BF16)
        nc.scalar.dma_start(out=shift_bf[:], in_=bp2.rearrange("(p t) -> p t", t=PACK))
        for g in STEPS[0]:
            load(g)
        w_rows = keep.tile([P, PACK, CHANNELS], BF16)
        w_source = wp2.rearrange("(p t) k -> p t k", t=PACK)
        for t in range(PACK):
            nc.sync.dma_start(out=w_rows[:, t, :], in_=w_source[:, t, :])
        key_rows = keep.tile([P, PACK, IMAGES, REGIONS], BF16)
        for s in range(1, LEAD):
            for g in STEPS[s]:
                load(g)
            if s == Q_LAG - 1:
                for n in range(IMAGES):
                    nc.sync.dma_start(out=key_rows[:, :, n, :], in_=key_obj[n].rearrange("(p j) m -> p j m", j=PACK))

        ident = keep.tile([P, P], F32)
        make_identity(nc, ident[:])
        gain = keep.tile([P, PACK], F32)
        nc.gpsimd.tensor_copy(out=gain[:], in_=gain_bf[:])
        shift = keep.tile([P, PACK], F32)
        nc.gpsimd.tensor_copy(out=shift[:], in_=shift_bf[:])

        def h_regroup_gpsimd(g):
            h_grouped = grouped.tile([P, WIDTHS[g], PACK], BF16, align_bytes=64)
            share = GPSIMD_SHARES[g]
            if share:
                nc.gpsimd.tensor_scalar(
                    out=h_grouped[:, :share, :],
                    in0=live["h_rows", g][:, :, :share].rearrange("p j w -> p w j"),
                    scalar1=1.0,
                    scalar2=0.0,
                    op0=ALU.mult,
                    op1=ALU.add,
                )
            live["h_grouped", g] = h_grouped

        def h_regroup_scalar(g):
            columns = slice(GPSIMD_SHARES[g], GPSIMD_SHARES[g] + SHARES[g])
            if SHARES[g]:
                regroup(nc.scalar.copy, live["h_grouped", g][:, columns, :], live["h_rows", g][:, :, columns])

        def h_regroup(g):
            rest = slice(GPSIMD_SHARES[g] + SHARES[g], WIDTHS[g])
            regroup(nc.vector.tensor_copy, live["h_grouped", g][:, rest, :], live.pop(("h_rows", g))[:, :, rest])

        def h_quantise(g):
            h_codes = work.tile([P, WIDTHS[g]], U32, align_bytes=64)
            h_scales = work.tile([P, WIDTHS[g]], U8, align_bytes=64)
            nc.vector.quantize_mx(
                out=h_codes[:].bitcast(FP8X4),
                scales=h_scales[:],
                in_=live.pop(("h_grouped", g))[:].rearrange("p w j -> p (w j)"),
            )
            live["h_mx", g] = (h_codes, h_scales)

        def w_quantise():
            w_words = w_rows[:].rearrange("p t k -> p (t k)").bitcast(F32).rearrange("p (t q u) -> p t u q", t=PACK, u=2)
            w_grouped = keep.tile([P, PACK, P * PACK], BF16, align_bytes=64)
            w_codes = keep.tile([P, PACK, P], U32, align_bytes=64)
            w_scales = keep.tile([P, PACK, P], U8, align_bytes=64)
            for t in range(PACK + 1):
                if t < PACK:
                    w_t = sim_banks.tile([P, 2, P], F32, tag="sim")
                    for u in range(2):
                        nc.tensor.transpose(w_t[:, u, :], w_words[:, t, u, :], ident[:])
                    nc.scalar.copy(
                        out=w_grouped[:, t, :].bitcast(F32).rearrange("p (o u) -> p o u", u=2),
                        in_=w_t[:].rearrange("p u o -> p o u"),
                    )
                if t > 0:
                    nc.vector.quantize_mx(
                        out=w_codes[:, t - 1, :].bitcast(FP8X4),
                        scales=w_scales[:, t - 1, :],
                        in_=w_grouped[:, t - 1, :],
                    )
            live["w_mx"] = (w_codes, w_scales)

        def project(g):
            if g == 0:
                w_quantise()
            w_codes, w_scales = live["w_mx"]
            h_codes, h_scales = live.pop(("h_mx", g))
            for column in range(0, WIDTHS[g], BANK):
                w = min(BANK, WIDTHS[g] - column)
                for t in range(PACK):
                    y = y_banks.tile([P, BANK], F32)
                    nc.tensor.matmul_mx(
                        out=y[:, :w],
                        lhsT=w_codes[:, t, :].bitcast(FP8X4),
                        lhsT_scale=w_scales[:, t, :],
                        rhs=h_codes[:, column : column + w].bitcast(FP8X4),
                        rhs_scale=h_scales[:, column : column + w],
                        start=True,
                        stop=True,
                    )
                    live["y", g, column, t] = y

        def leave_psum(g):
            q_rows = query.tile([P, PACK, WIDTHS[g]], BF16)
            for column in range(0, WIDTHS[g], BANK):
                w = min(BANK, WIDTHS[g] - column)
                for t in range(PACK):
                    nc.scalar.activation(
                        out=q_rows[:, t, column : column + w],
                        in_=live.pop(("y", g, column, t))[:, :w],
                        func=ACT.Relu,
                        bias=shift[:, t : t + 1],
                        scale=gain[:, t : t + 1],
                    )
            live["q_rows", g] = q_rows

        def q_regroup(g):
            q_grouped = work.tile([P, WIDTHS[g], PACK], BF16, align_bytes=64)
            regroup(nc.vector.tensor_copy, q_grouped[:], live.pop(("q_rows", g))[:])
            live["q_grouped", g] = q_grouped

        def q_quantise(g):
            q_codes = work.tile([P, WIDTHS[g]], U32, align_bytes=64)
            q_scales = work.tile([P, WIDTHS[g]], U8, align_bytes=64)
            nc.vector.quantize_mx(
                out=q_codes[:].bitcast(FP8X4),
                scales=q_scales[:],
                in_=live.pop(("q_grouped", g))[:].rearrange("p w j -> p (w j)"),
            )
            live["q_mx", g] = (q_codes, q_scales)

        key_grouped = keep.tile([P, IMAGES * REGIONS, PACK], BF16, align_bytes=64)
        live["key_grouped"] = key_grouped

        def key_regroup():
            regroup(nc.vector.tensor_copy, key_grouped[:], key_rows[:].rearrange("p j n m -> p j (n m)"))

        def key_quantise():
            key_codes = keep.tile([P, IMAGES * REGIONS], U32, align_bytes=64)
            key_scales = keep.tile([P, IMAGES * REGIONS], U8, align_bytes=64)
            nc.vector.quantize_mx(
                out=key_codes[:].bitcast(FP8X4),
                scales=key_scales[:],
                in_=live.pop("key_grouped")[:].rearrange("p m j -> p (m j)"),
            )
            live["key_mx"] = (key_codes, key_scales)

        def scores(g):
            key_codes, key_scales = live["key_mx"]
            q_codes, q_scales = live.pop(("q_mx", g))
            for column in range(0, WIDTHS[g], BANK):
                w = min(BANK, WIDTHS[g] - column)
                sim = sim_banks.tile([P, BANK // P, REGIONS], F32, tag="sim")
                for i in range(w // P):
                    first = column + i * P
                    n = (STARTS[g] + first) // PIXELS
                    nc.tensor.matmul_mx(
                        out=sim[:, i, :],
                        lhsT=q_codes[:, first : first + P].bitcast(FP8X4),
                        lhsT_scale=q_scales[:, first : first + P],
                        rhs=key_codes[:, n * REGIONS : (n + 1) * REGIONS].bitcast(FP8X4),
                        rhs_scale=key_scales[:, n * REGIONS : (n + 1) * REGIONS],
                        start=True,
                        stop=True,
                    )
                live["sim", g, column] = sim

        def row_max(g):
            top = small.tile([P, WIDTHS[g] // P], F32)
            for column in range(0, WIDTHS[g], BANK):
                w = min(BANK, WIDTHS[g] - column)
                nc.vector.tensor_reduce(
                    out=top[:, column // P : (column + w) // P],
                    in_=live["sim", g, column][:, : w // P, :],
                    axis=AXIS.X,
                    op=ALU.max,
                )
            live["top", g] = top

        def row_shift(g):
            minus_top = small.tile([P, WIDTHS[g] // P], F32)
            nc.scalar.activation(out=minus_top[:], in_=live.pop(("top", g))[:], func=ACT.Copy, scale=-SIM_SCALE)
            live["minus_top", g] = minus_top

        def exponent(g):
            minus_top = live.pop(("minus_top", g))
            e = result.tile([P, WIDTHS[g] // P, REGIONS], F32)
            sums = small.tile([P, WIDTHS[g] // P], F32)
            for column in range(0, WIDTHS[g], BANK):
                sim = live.pop(("sim", g, column))
                for i in range(min(BANK, WIDTHS[g] - column) // P):
                    j = column // P + i
                    nc.scalar.activation(
                        out=e[:, j, :],
                        in_=sim[:, i, :],
                        func=ACT.Exp,
                        bias=minus_top[:, j : j + 1],
                        scale=SIM_SCALE,
                        accum_out=sums[:, j : j + 1],
                    )
            live["e", g] = e
            live["sums", g] = sums

        def invert_sums(g):
            inverse = small.tile([P, WIDTHS[g] // P], F32)
            nc.vector.reciprocal(out=inverse[:], in_=live.pop(("sums", g))[:])
            live["inverse", g] = inverse

        def normalise(g):
            e = live.pop(("e", g))
            inverse = live.pop(("inverse", g))
            tiles = WIDTHS[g] // P
            for j in range(tiles):
                if g >= len(WIDTHS) - VECTOR_ENDS:
                    nc.vector.tensor_scalar_mul(out=e[:, j, :], in0=e[:, j, :], scalar1=inverse[:, j : j + 1])
                else:
                    nc.scalar.activation(out=e[:, j, :], in_=e[:, j, :], func=ACT.Copy, scale=inverse[:, j : j + 1])
            for n, pixel, column, w in pieces(g, BANK):
                nc.sync.dma_start(
                    out=out[n, pixel : pixel + w, :].rearrange("(i p) m -> p i m", p=P),
                    in_=e[:, column // P : (column + w) // P, :],
                )

        def at(stage, s):
            if 0 <= s < len(STEPS):
                for g in STEPS[s]:
                    stage(g)

        for s in range(GROUPED_BUFS):
            at(h_regroup_gpsimd, s)
        at(h_regroup_scalar, 0)
        for s in range(len(STEPS) + DEPTH):
            at(load, s + LEAD)
            at(leave_psum, s - 1)
            if s < TAILSTEP:
                at(row_max, s - Q_LAG - 1)
            at(q_regroup, s - Q_LAG)
            if s >= TAILSTEP:
                at(row_max, s - Q_LAG - 1)
            if s == Q_LAG - 1:
                key_regroup()
            at(h_regroup, s)
            if s == Q_LAG:
                key_quantise()
            at(q_quantise, s - Q_LAG)
            at(scores, s - Q_LAG)
            at(invert_sums, s - Q_LAG - 2)
            at(h_quantise, s)
            at(h_regroup_gpsimd, s + GROUPED_BUFS)
            at(project, s)
            at(row_shift, s - Q_LAG - 1)
            at(exponent, s - Q_LAG - 1)
            at(normalise, s - Q_LAG - 2)
            at(h_regroup_scalar, s + 1)
